import numpy as np
import ml_dtypes


def mxq(x, axis, fmt="e4m3"):
    dtype, down = {"e4m3": (ml_dtypes.float8_e4m3fn, 7), "e5m2": (ml_dtypes.float8_e5m2, 14)}[fmt]
    v = np.moveaxis(np.asarray(x, np.float32).astype(ml_dtypes.bfloat16).astype(np.float64), axis, -1)
    blocks = v.reshape(v.shape[:-1] + (-1, 32))
    amax = np.abs(blocks).max(-1, keepdims=True)
    byte = np.maximum(np.where(amax > 0, np.frexp(amax)[1] - 1 + 127, 0) - down, 1)
    scale = np.exp2(byte - 127.0)
    codes = (blocks / scale).astype(np.float32).astype(dtype).astype(np.float64)
    return np.moveaxis((codes * scale).reshape(v.shape), -1, axis)


WIDE = False


def mx_kscale(k):
    if not WIDE:
        return np.ones(k)
    levels = np.array([20, -20, 10, -10, 0])
    a = np.random.permutation(np.resize(levels, k // 512 * 4)).reshape(k // 512, 4)
    idx = np.arange(k)
    return np.exp2(a[idx // 512, idx % 128 // 32])


BF16 = ml_dtypes.bfloat16


def bf(x):
    return np.asarray(x, np.float32).astype(BF16)


def f64(x):
    return np.asarray(x).astype(np.float64)


T, B, I, H = 16, 128, 512, 512


def sigmoid(v):
    return 1.0 / (1.0 + np.exp(-v))


def setup_inputs():
    s = mx_kscale(T * B).reshape(T, B, 1)
    x0 = bf(np.random.standard_normal((T, B, I)))
    h0 = bf(np.random.standard_normal((B, H)))
    c0 = bf(np.random.standard_normal((B, H)))
    noise = bf(np.random.standard_normal((B, H)) * 0.3)
    W_ih = bf(np.random.standard_normal((4 * H, I)) / np.sqrt(I))
    W_hh = bf(np.random.standard_normal((4 * H, H)) * 0.7 / np.sqrt(H))
    b_ih = bf(np.random.standard_normal(4 * H) * 0.3)
    b_hh = bf(np.random.standard_normal(4 * H) * 0.3)
    g = bf(np.random.standard_normal((T, B, H)) * np.exp2(np.random.randint(-12, 1, (T, B, 1))) * 4.0 / s)
    gates = f64(x0) @ f64(W_ih).T + (f64(h0) @ f64(W_hh).T)[None, :, :] + (f64(b_ih) + f64(b_hh))
    return {
        "input": bf(f64(x0) * s),
        "h0": h0,
        "c0": c0,
        "noise": noise,
        "W_ih": W_ih,
        "W_hh": W_hh,
        "b_ih": b_ih,
        "b_hh": b_hh,
        "gates": np.asarray(gates, np.float32),
        "grad_out": g,
    }


def reference(input, h0, c0, noise, W_ih, W_hh, b_ih, b_hh, gates, grad_out):
    hsz = c0.shape[-1]
    a = f64(gates)
    go = f64(grad_out)
    c0f = f64(c0)[None]
    i_g = sigmoid(a[..., 0 * hsz:1 * hsz])
    f_g = sigmoid(a[..., 1 * hsz:2 * hsz])
    g_g = np.tanh(a[..., 2 * hsz:3 * hsz])
    o_g = sigmoid(a[..., 3 * hsz:4 * hsz])
    c = f_g * c0f + i_g * g_g
    tc = np.tanh(c)
    dc = go * o_g * (1.0 - tc * tc)
    da_i = dc * g_g * i_g * (1.0 - i_g)
    da_f = dc * c0f * f_g * (1.0 - f_g)
    da_g = dc * i_g * (1.0 - g_g * g_g)
    da_o = go * tc * o_g * (1.0 - o_g)
    dgates = np.concatenate([da_i, da_f, da_g, da_o], axis=-1)
    n = dgates.shape[0] * dgates.shape[1]
    d2 = dgates.reshape(n, 4 * hsz)
    x2 = f64(input).reshape(n, -1)
    return mxq(d2, 0, "e5m2").T @ mxq(x2, 0, "e4m3")

@@ -1,0 +1,203 @@
+from contextlib import ExitStack
+
+import concourse.mybir as mybir
+
+F32 = mybir.dt.float32
+BF16 = mybir.dt.bfloat16
+U32 = mybir.dt.uint32
+U8 = mybir.dt.uint8
+E4M3_X4 = mybir.dt.float8_e4m3fn_x4
+E5M2_X4 = mybir.dt.float8_e5m2_x4
+ACT = mybir.ActivationFunctionType
+ALU = mybir.AluOpType
+
+P = 128
+PACK = 4
+K_PASS = P * PACK
+BATCH = 128
+TOKENS = 16 * BATCH
+PASSES = TOKENS // K_PASS
+H = 512
+N_IN = 512
+GATES = ("i", "f", "g", "o")
+ROUNDS = 2
+H_ROUND = H // ROUNDS
+M_TILES = H_ROUND // P
+COLS = H_ROUND * PACK
+CHUNKS = ROUNDS * PASSES
+
+FLOPS = 2 * TOKENS * (4 * H) * N_IN
+BYTES = TOKENS * 4 * H * 4 + 2 * TOKENS * H * 2 + BATCH * H * 2 + 4 * H * N_IN * 4
+
+
+def tile_lstmlayer_v_kernel(
+    tc, x, h0, c0, noise, w_ih, w_hh, b_ih, b_hh, gates, grad_out, out
+):
+    nc = tc.nc
+    gates_rows = gates.flatten_outer_dims()
+    grad_rows = grad_out.flatten_outer_dims()
+    x_rows = x.flatten_outer_dims()
+
+    def by_partition(rows):
+        return rows.rearrange("(p j) w -> p j w", j=PACK)
+
+    def tokens_innermost(loaded):
+        return loaded.rearrange("p j w -> p w j")
+
+    def as_words(flat):
+        return flat.rearrange("p (w j) -> p w j", j=PACK)
+
+    with ExitStack() as stack:
+        keep = stack.enter_context(tc.tile_pool(name="keep", bufs=1))
+        loads = stack.enter_context(tc.tile_pool(name="loads", bufs=2))
+        work = stack.enter_context(tc.tile_pool(name="work", bufs=2))
+        psum = stack.enter_context(tc.psum_pool(name="psum", bufs=1))
+        c0_loaded = keep.tile([P, PACK, H], BF16)
+        c0_words = keep.tile([P, H * PACK], BF16)
+        x_codes = keep.tile([P, PASSES, N_IN], U32, align_bytes=64)
+        x_scales = keep.tile([P, PASSES, N_IN], U8, align_bytes=64)
+
+        def load_chunk(n):
+            rnd, g = divmod(n, PASSES)
+            tokens = slice(g * K_PASS, (g + 1) * K_PASS)
+            loaded = {}
+            for gate in ("i", "g", "f", "o"):
+                first = GATES.index(gate) * H + rnd * H_ROUND
+                loaded[gate] = loads.tile([P, PACK, H_ROUND], F32, name="loaded_" + gate)
+                nc.sync.dma_start(
+                    out=loaded[gate][:],
+                    in_=by_partition(gates_rows[tokens, first : first + H_ROUND]),
+                )
+            loaded["grad"] = loads.tile([P, PACK, H_ROUND], BF16, name="loaded_grad")
+            nc.sync.dma_start(
+                out=loaded["grad"][:],
+                in_=by_partition(grad_rows[tokens, rnd * H_ROUND : (rnd + 1) * H_ROUND]),
+            )
+            if rnd == 0:
+                loaded["x"] = loads.tile([P, PACK, N_IN], BF16, name="loaded_x")
+                nc.sync.dma_start(out=loaded["x"][:], in_=by_partition(x_rows[tokens, :]))
+            return loaded
+
+        def scalar_front(loaded):
+            t = {}
+            for gate, func in (("i", ACT.Sigmoid), ("g", ACT.Tanh), ("f", ACT.Sigmoid), ("o", ACT.Sigmoid)):
+                t[gate] = work.tile([P, COLS], F32, name="act_" + gate)
+                nc.scalar.activation(
+                    out=as_words(t[gate][:]), in_=tokens_innermost(loaded[gate][:]), func=func
+                )
+            t["grad"] = work.tile([P, COLS], BF16, name="grad_words")
+            nc.scalar.copy(out=as_words(t["grad"][:]), in_=tokens_innermost(loaded["grad"][:]))
+            t["g2"] = work.tile([P, COLS], F32, name="g_squared")
+            nc.scalar.activation(out=t["g2"][:], in_=t["g"][:], func=ACT.Square)
+            if "x" in loaded:
+                t["x"] = work.tile([P, N_IN * PACK], BF16, name="x_words", align_bytes=64)
+                nc.scalar.copy(out=as_words(t["x"][:]), in_=tokens_innermost(loaded["x"][:]))
+            return t
+
+        def vector_front(n, t):
+            rnd, g = divmod(n, PASSES)
+
+            def minus_one_times(name, in0, in1):
+                t[name] = work.tile([P, COLS], F32, name=name)
+                nc.vector.scalar_tensor_tensor(
+                    out=t[name][:], in0=in0[:], scalar=1.0, in1=in1[:], op0=ALU.subtract, op1=ALU.mult
+                )
+
+            v = work.tile([P, COLS], F32, bufs=1)
+            u = work.tile([P, COLS], F32, bufs=1)
+            t["w"] = work.tile([P, COLS], F32, name="w")
+            t["c"] = work.tile([P, COLS], F32, name="c", bufs=1)
+            c0_chunk = c0_words[:, rnd * COLS : (rnd + 1) * COLS]
+            nc.vector.tensor_tensor(out=v[:], in0=t["i"][:], in1=t["g"][:], op=ALU.mult)
+            nc.vector.tensor_tensor(out=u[:], in0=t["f"][:], in1=c0_chunk, op=ALU.mult)
+            nc.vector.tensor_tensor(out=t["w"][:], in0=t["o"][:], in1=t["grad"][:], op=ALU.mult)
+            nc.vector.tensor_tensor(out=t["c"][:], in0=u[:], in1=v[:], op=ALU.add)
+            minus_one_times("np_i", t["i"], v)
+            minus_one_times("np_f", t["f"], u)
+            minus_one_times("ny", t["o"], t["w"])
+            minus_one_times("np_g", t["g2"], t["i"])
+            if "x" in t:
+                nc.vector.quantize_mx(
+                    out=x_codes[:, g, :].bitcast(E4M3_X4), scales=x_scales[:, g, :], in_=t["x"][:]
+                )
+
+        def scalar_middle(t):
+            t["ntc"] = work.tile([P, COLS], F32, name="ntc")
+            nc.scalar.activation(out=t["ntc"][:], in_=t["c"][:], func=ACT.Tanh, scale=-1.0)
+            t["tc2"] = work.tile([P, COLS], F32, name="tc_squared")
+            nc.scalar.activation(out=t["tc2"][:], in_=t["ntc"][:], func=ACT.Square)
+
+        def back(n, t, acc):
+            rnd, g = divmod(n, PASSES)
+            da = {}
+            codes = {}
+            scales = {}
+
+            def product(gate, in0, in1):
+                da[gate] = work.tile([P, COLS], BF16, name="da_" + gate, bufs=1, align_bytes=64)
+                nc.vector.tensor_tensor(out=da[gate][:], in0=in0[:], in1=in1[:], op=ALU.mult)
+
+            def quantise_and_multiply(gate):
+                codes[gate] = work.tile([P, H_ROUND], U32, name="codes_" + gate, align_bytes=64)
+                scales[gate] = work.tile([P, H_ROUND], U8, name="scales_" + gate, align_bytes=64)
+                nc.vector.quantize_mx(
+                    out=codes[gate][:].bitcast(E5M2_X4), scales=scales[gate][:], in_=da[gate][:]
+                )
+                for m in range(M_TILES):
+                    m_cols = slice(m * P, (m + 1) * P)
+                    nc.tensor.matmul_mx(
+                        out=acc[gate][m][:],
+                        lhsT=codes[gate][:, m_cols].bitcast(E5M2_X4),
+                        lhsT_scale=scales[gate][:, m_cols],
+                        rhs=x_codes[:, g, :].bitcast(E4M3_X4),
+                        rhs_scale=x_scales[:, g, :],
+                        start=(g == 0),
+                        stop=(g == PASSES - 1),
+                    )
+                if g == PASSES - 1:
+                    result = work.tile([P, M_TILES, N_IN], F32, name="result", bufs=len(GATES))
+                    for m in range(M_TILES):
+                        nc.scalar.copy(out=result[:, m, :], in_=acc[gate][m][:])
+                    first = GATES.index(gate) * H + rnd * H_ROUND
+                    nc.scalar.dma_start(
+                        out=out[first : first + H_ROUND, :].rearrange("(m p) n -> p m n", p=P),
+                        in_=result[:],
+                    )
+
+            ndc = work.tile([P, COLS], F32, bufs=1)
+            nc.vector.scalar_tensor_tensor(
+                out=ndc[:], in0=t["tc2"][:], scalar=1.0, in1=t["w"][:], op0=ALU.subtract, op1=ALU.mult
+            )
+            product("o", t["ny"], t["ntc"])
+            product("i", t["np_i"], ndc)
+            quantise_and_multiply("o")
+            product("f", t["np_f"], ndc)
+            quantise_and_multiply("i")
+            product("g", t["np_g"], ndc)
+            quantise_and_multiply("f")
+            quantise_and_multiply("g")
+
+        for first_p in range(0, P, BATCH // PACK):
+            nc.scalar.dma_start(
+                out=c0_loaded[first_p : first_p + BATCH // PACK], in_=by_partition(c0[:, :])
+            )
+        first_loads = load_chunk(0)
+        nc.vector.tensor_copy(out=as_words(c0_words[:]), in_=tokens_innermost(c0_loaded[:]))
+
+        tiles = {0: scalar_front(first_loads)}
+        vector_front(0, tiles[0])
+        tiles[1] = scalar_front(load_chunk(1))
+        scalar_middle(tiles[0])
+        acc = {}
+        for n in range(CHUNKS):
+            if n + 2 < CHUNKS:
+                tiles[n + 2] = scalar_front(load_chunk(n + 2))
+            if n + 1 < CHUNKS:
+                vector_front(n + 1, tiles[n + 1])
+                scalar_middle(tiles[n + 1])
+            if n % PASSES == 0:
+                for gate in GATES:
+                    acc[gate] = [
+                        psum.tile([P, N_IN], F32, name="acc_%s%d" % (gate, m)) for m in range(M_TILES)
+                    ]
+            back(n, tiles[n], acc)

@@ -1,6 +1,7 @@
 from contextlib import ExitStack
 
 import concourse.mybir as mybir
+from concourse.masks import make_identity
 
 F32 = mybir.dt.float32
 BF16 = mybir.dt.bfloat16
@@ -20,11 +21,14 @@ PASSES = TOKENS // K_PASS
 H = 512
 N_IN = 512
 GATES = ("i", "f", "g", "o")
-ROUNDS = 2
-H_ROUND = H // ROUNDS
-M_TILES = H_ROUND // P
-COLS = H_ROUND * PACK
-CHUNKS = ROUNDS * PASSES
+H_ROUND = P
+ROUNDS = H // H_ROUND
+CHUNK_PASSES = 2
+ROUND_CHUNKS = PASSES // CHUNK_PASSES
+CHUNKS = ROUNDS * ROUND_CHUNKS
+PASS_COLS = H_ROUND * PACK
+COLS = CHUNK_PASSES * PASS_COLS
+PLAIN_ROUNDS = 3
 
 FLOPS = 2 * TOKENS * (4 * H) * N_IN
 BYTES = TOKENS * 4 * H * 4 + 2 * TOKENS * H * 2 + BATCH * H * 2 + 4 * H * N_IN * 4
@@ -42,40 +46,46 @@ def tile_lstmlayer_v_kernel(
         return rows.rearrange("(p j) w -> p j w", j=PACK)
 
     def tokens_innermost(loaded):
-        return loaded.rearrange("p j w -> p w j")
+        return loaded.rearrange("p s j w -> p s w j")
 
     def as_words(flat):
-        return flat.rearrange("p (w j) -> p w j", j=PACK)
+        return flat.rearrange("p (s w j) -> p s w j", s=CHUNK_PASSES, j=PACK)
 
     with ExitStack() as stack:
         keep = stack.enter_context(tc.tile_pool(name="keep", bufs=1))
         loads = stack.enter_context(tc.tile_pool(name="loads", bufs=2))
         work = stack.enter_context(tc.tile_pool(name="work", bufs=2))
         psum = stack.enter_context(tc.psum_pool(name="psum", bufs=1))
+        stack.enter_context(tc.manual_schedule())
         c0_loaded = keep.tile([P, PACK, H], BF16)
         c0_words = keep.tile([P, H * PACK], BF16)
         x_codes = keep.tile([P, PASSES, N_IN], U32, align_bytes=64)
         x_scales = keep.tile([P, PASSES, N_IN], U8, align_bytes=64)
+        identity = keep.tile([P, P], F32)
+        make_identity(nc, identity[:])
+
+        def load(n, loaded, names):
+            rnd, part = divmod(n, ROUND_CHUNKS)
+            for name in names:
+                if name == "x":
+                    rows, first, width, dtype = x_rows, 0, N_IN, BF16
+                elif name == "grad":
+                    rows, first, width, dtype = grad_rows, rnd * H_ROUND, H_ROUND, BF16
+                else:
+                    rows, first, width, dtype = gates_rows, GATES.index(name) * H + rnd * H_ROUND, H_ROUND, F32
+                loaded[name] = loads.tile([P, CHUNK_PASSES, PACK, width], dtype, name="loaded_" + name)
+                for s in range(CHUNK_PASSES):
+                    g = part * CHUNK_PASSES + s
+                    nc.sync.dma_start(
+                        out=loaded[name][:, s],
+                        in_=by_partition(rows[g * K_PASS : (g + 1) * K_PASS, first : first + width]),
+                    )
 
         def load_chunk(n):
-            rnd, g = divmod(n, PASSES)
-            tokens = slice(g * K_PASS, (g + 1) * K_PASS)
             loaded = {}
-            for gate in ("i", "g", "f", "o"):
-                first = GATES.index(gate) * H + rnd * H_ROUND
-                loaded[gate] = loads.tile([P, PACK, H_ROUND], F32, name="loaded_" + gate)
-                nc.sync.dma_start(
-                    out=loaded[gate][:],
-                    in_=by_partition(gates_rows[tokens, first : first + H_ROUND]),
-                )
-            loaded["grad"] = loads.tile([P, PACK, H_ROUND], BF16, name="loaded_grad")
-            nc.sync.dma_start(
-                out=loaded["grad"][:],
-                in_=by_partition(grad_rows[tokens, rnd * H_ROUND : (rnd + 1) * H_ROUND]),
-            )
-            if rnd == 0:
-                loaded["x"] = loads.tile([P, PACK, N_IN], BF16, name="loaded_x")
-                nc.sync.dma_start(out=loaded["x"][:], in_=by_partition(x_rows[tokens, :]))
+            load(n, loaded, ("i", "g", "f", "o", "grad"))
+            if n < ROUND_CHUNKS:
+                load(n, loaded, ("x",))
             return loaded
 
         def scalar_front(loaded):
@@ -89,13 +99,10 @@ def tile_lstmlayer_v_kernel(
             nc.scalar.copy(out=as_words(t["grad"][:]), in_=tokens_innermost(loaded["grad"][:]))
             t["g2"] = work.tile([P, COLS], F32, name="g_squared")
             nc.scalar.activation(out=t["g2"][:], in_=t["g"][:], func=ACT.Square)
-            if "x" in loaded:
-                t["x"] = work.tile([P, N_IN * PACK], BF16, name="x_words", align_bytes=64)
-                nc.scalar.copy(out=as_words(t["x"][:]), in_=tokens_innermost(loaded["x"][:]))
             return t
 
         def vector_front(n, t):
-            rnd, g = divmod(n, PASSES)
+            rnd = n // ROUND_CHUNKS
 
             def minus_one_times(name, in0, in1):
                 t[name] = work.tile([P, COLS], F32, name=name)
@@ -106,63 +113,58 @@ def tile_lstmlayer_v_kernel(
             v = work.tile([P, COLS], F32, bufs=1)
             u = work.tile([P, COLS], F32, bufs=1)
             t["w"] = work.tile([P, COLS], F32, name="w")
-            t["c"] = work.tile([P, COLS], F32, name="c", bufs=1)
-            c0_chunk = c0_words[:, rnd * COLS : (rnd + 1) * COLS]
+            c0_round = c0_words[:, rnd * PASS_COLS : (rnd + 1) * PASS_COLS]
             nc.vector.tensor_tensor(out=v[:], in0=t["i"][:], in1=t["g"][:], op=ALU.mult)
-            nc.vector.tensor_tensor(out=u[:], in0=t["f"][:], in1=c0_chunk, op=ALU.mult)
+            nc.vector.tensor_tensor(
+                out=u[:].rearrange("p (s c) -> p s c", s=CHUNK_PASSES),
+                in0=t["f"][:].rearrange("p (s c) -> p s c", s=CHUNK_PASSES),
+                in1=c0_round.unsqueeze(1).to_broadcast([P, CHUNK_PASSES, PASS_COLS]),
+                op=ALU.mult,
+            )
             nc.vector.tensor_tensor(out=t["w"][:], in0=t["o"][:], in1=t["grad"][:], op=ALU.mult)
-            nc.vector.tensor_tensor(out=t["c"][:], in0=u[:], in1=v[:], op=ALU.add)
+            pass_cols = [slice(s * PASS_COLS, (s + 1) * PASS_COLS) for s in range(CHUNK_PASSES)]
+            if rnd < PLAIN_ROUNDS:
+                t["c"] = []
+                for cols in pass_cols:
+                    c_bank = psum.tile([P, PASS_COLS], F32, name="c_bank", bufs=2 * CHUNK_PASSES)
+                    nc.tensor.matmul(out=c_bank[:], lhsT=identity[:], rhs=u[:, cols], start=True, stop=False)
+                    nc.tensor.matmul(out=c_bank[:], lhsT=identity[:], rhs=v[:, cols], start=False, stop=True)
+                    t["c"].append(c_bank[:])
+            else:
+                c = work.tile([P, COLS], F32, bufs=1)
+                nc.vector.tensor_tensor(out=c[:], in0=u[:], in1=v[:], op=ALU.add)
+                t["c"] = [c[:, cols] for cols in pass_cols]
             minus_one_times("np_i", t["i"], v)
             minus_one_times("np_f", t["f"], u)
             minus_one_times("ny", t["o"], t["w"])
             minus_one_times("np_g", t["g2"], t["i"])
-            if "x" in t:
-                nc.vector.quantize_mx(
-                    out=x_codes[:, g, :].bitcast(E4M3_X4), scales=x_scales[:, g, :], in_=t["x"][:]
-                )
 
-        def scalar_middle(t):
+        def scalar_middle(t, loaded):
             t["ntc"] = work.tile([P, COLS], F32, name="ntc")
-            nc.scalar.activation(out=t["ntc"][:], in_=t["c"][:], func=ACT.Tanh, scale=-1.0)
+            for s in range(CHUNK_PASSES):
+                nc.scalar.activation(
+                    out=t["ntc"][:, s * PASS_COLS : (s + 1) * PASS_COLS], in_=t["c"][s], func=ACT.Tanh, scale=-1.0
+                )
             t["tc2"] = work.tile([P, COLS], F32, name="tc_squared")
             nc.scalar.activation(out=t["tc2"][:], in_=t["ntc"][:], func=ACT.Square)
+            if "x" in loaded:
+                t["x"] = work.tile([P, CHUNK_PASSES * N_IN * PACK], BF16, name="x_words", align_bytes=64)
+                nc.scalar.copy(out=as_words(t["x"][:]), in_=tokens_innermost(loaded["x"][:]))
 
-        def back(n, t, acc):
-            rnd, g = divmod(n, PASSES)
+        def vector_back(n, t):
+            part = n % ROUND_CHUNKS
             da = {}
-            codes = {}
-            scales = {}
 
             def product(gate, in0, in1):
                 da[gate] = work.tile([P, COLS], BF16, name="da_" + gate, bufs=1, align_bytes=64)
                 nc.vector.tensor_tensor(out=da[gate][:], in0=in0[:], in1=in1[:], op=ALU.mult)
 
-            def quantise_and_multiply(gate):
-                codes[gate] = work.tile([P, H_ROUND], U32, name="codes_" + gate, align_bytes=64)
-                scales[gate] = work.tile([P, H_ROUND], U8, name="scales_" + gate, align_bytes=64)
+            def quantise(gate):
+                t["codes_" + gate] = work.tile([P, COLS // PACK], U32, name="codes_" + gate, align_bytes=64)
+                t["scales_" + gate] = work.tile([P, COLS // PACK], U8, name="scales_" + gate, align_bytes=64)
                 nc.vector.quantize_mx(
-                    out=codes[gate][:].bitcast(E5M2_X4), scales=scales[gate][:], in_=da[gate][:]
+                    out=t["codes_" + gate][:].bitcast(E5M2_X4), scales=t["scales_" + gate][:], in_=da[gate][:]
                 )
-                for m in range(M_TILES):
-                    m_cols = slice(m * P, (m + 1) * P)
-                    nc.tensor.matmul_mx(
-                        out=acc[gate][m][:],
-                        lhsT=codes[gate][:, m_cols].bitcast(E5M2_X4),
-                        lhsT_scale=scales[gate][:, m_cols],
-                        rhs=x_codes[:, g, :].bitcast(E4M3_X4),
-                        rhs_scale=x_scales[:, g, :],
-                        start=(g == 0),
-                        stop=(g == PASSES - 1),
-                    )
-                if g == PASSES - 1:
-                    result = work.tile([P, M_TILES, N_IN], F32, name="result", bufs=len(GATES))
-                    for m in range(M_TILES):
-                        nc.scalar.copy(out=result[:, m, :], in_=acc[gate][m][:])
-                    first = GATES.index(gate) * H + rnd * H_ROUND
-                    nc.scalar.dma_start(
-                        out=out[first : first + H_ROUND, :].rearrange("(m p) n -> p m n", p=P),
-                        in_=result[:],
-                    )
 
             ndc = work.tile([P, COLS], F32, bufs=1)
             nc.vector.scalar_tensor_tensor(
@@ -170,34 +172,67 @@ def tile_lstmlayer_v_kernel(
             )
             product("o", t["ny"], t["ntc"])
             product("i", t["np_i"], ndc)
-            quantise_and_multiply("o")
+            quantise("o")
             product("f", t["np_f"], ndc)
-            quantise_and_multiply("i")
+            quantise("i")
             product("g", t["np_g"], ndc)
-            quantise_and_multiply("f")
-            quantise_and_multiply("g")
+            quantise("f")
+            quantise("g")
+            if "x" in t:
+                chunk_passes = slice(part * CHUNK_PASSES, (part + 1) * CHUNK_PASSES)
+                nc.vector.quantize_mx(
+                    out=x_codes[:, chunk_passes, :].rearrange("p s n -> p (s n)").bitcast(E4M3_X4),
+                    scales=x_scales[:, chunk_passes, :].rearrange("p s n -> p (s n)"),
+                    in_=t["x"][:],
+                )
 
+        def multiply(n, t, acc):
+            rnd, part = divmod(n, ROUND_CHUNKS)
+            for gate in ("o", "i", "f", "g"):
+                for s in range(CHUNK_PASSES):
+                    g = part * CHUNK_PASSES + s
+                    m_cols = slice(s * H_ROUND, (s + 1) * H_ROUND)
+                    nc.tensor.matmul_mx(
+                        out=acc[gate][:],
+                        lhsT=t["codes_" + gate][:, m_cols].bitcast(E5M2_X4),
+                        lhsT_scale=t["scales_" + gate][:, m_cols],
+                        rhs=x_codes[:, g, :].bitcast(E4M3_X4),
+                        rhs_scale=x_scales[:, g, :],
+                        start=(g == 0),
+                        stop=(g == PASSES - 1),
+                    )
+                if part == ROUND_CHUNKS - 1:
+                    result = work.tile([P, N_IN], F32, name="result", bufs=len(GATES))
+                    nc.scalar.copy(out=result[:], in_=acc[gate][:])
+                    first = GATES.index(gate) * H + rnd * H_ROUND
+                    nc.scalar.dma_start(out=out[first : first + H_ROUND, :], in_=result[:])
+
+        loaded = {0: {}}
+        load(0, loaded[0], ("i", "g"))
         for first_p in range(0, P, BATCH // PACK):
-            nc.scalar.dma_start(
+            nc.sync.dma_start(
                 out=c0_loaded[first_p : first_p + BATCH // PACK], in_=by_partition(c0[:, :])
             )
-        first_loads = load_chunk(0)
-        nc.vector.tensor_copy(out=as_words(c0_words[:]), in_=tokens_innermost(c0_loaded[:]))
+        load(0, loaded[0], ("f", "o", "grad", "x"))
+        nc.vector.tensor_copy(
+            out=c0_words[:].rearrange("p (w j) -> p w j", j=PACK), in_=c0_loaded[:].rearrange("p j w -> p w j")
+        )
 
-        tiles = {0: scalar_front(first_loads)}
+        tiles = {0: scalar_front(loaded[0])}
         vector_front(0, tiles[0])
-        tiles[1] = scalar_front(load_chunk(1))
-        scalar_middle(tiles[0])
+        loaded[1] = load_chunk(1)
+        tiles[1] = scalar_front(loaded[1])
+        scalar_middle(tiles[0], loaded[0])
         acc = {}
         for n in range(CHUNKS):
             if n + 2 < CHUNKS:
-                tiles[n + 2] = scalar_front(load_chunk(n + 2))
+                loaded[n + 2] = load_chunk(n + 2)
+                tiles[n + 2] = scalar_front(loaded[n + 2])
             if n + 1 < CHUNKS:
                 vector_front(n + 1, tiles[n + 1])
-                scalar_middle(tiles[n + 1])
-            if n % PASSES == 0:
+                scalar_middle(tiles[n + 1], loaded[n + 1])
+            vector_back(n, tiles[n])
+            if n % ROUND_CHUNKS == 0:
                 for gate in GATES:
-                    acc[gate] = [
-                        psum.tile([P, N_IN], F32, name="acc_%s%d" % (gate, m)) for m in range(M_TILES)
-                    ]
-            back(n, tiles[n], acc)
+                    acc[gate] = psum.tile([P, N_IN], F32, name="acc_" + gate)
+            multiply(n, tiles[n], acc)

@@ -58,7 +58,6 @@ def tile_lstmlayer_v_kernel(
         psum = stack.enter_context(tc.psum_pool(name="psum", bufs=1))
         stack.enter_context(tc.manual_schedule())
         c0_loaded = keep.tile([P, PACK, H], BF16)
-        c0_words = keep.tile([P, H * PACK], BF16)
         x_codes = keep.tile([P, PASSES, N_IN], U32, align_bytes=64)
         x_scales = keep.tile([P, PASSES, N_IN], U8, align_bytes=64)
         identity = keep.tile([P, P], F32)
@@ -95,13 +94,11 @@ def tile_lstmlayer_v_kernel(
                 nc.scalar.activation(
                     out=as_words(t[gate][:]), in_=tokens_innermost(loaded[gate][:]), func=func
                 )
-            t["grad"] = work.tile([P, COLS], BF16, name="grad_words")
-            nc.scalar.copy(out=as_words(t["grad"][:]), in_=tokens_innermost(loaded["grad"][:]))
             t["g2"] = work.tile([P, COLS], F32, name="g_squared")
             nc.scalar.activation(out=t["g2"][:], in_=t["g"][:], func=ACT.Square)
             return t
 
-        def vector_front(n, t):
+        def vector_front(n, t, loaded):
             rnd = n // ROUND_CHUNKS
 
             def minus_one_times(name, in0, in1):
@@ -113,15 +110,20 @@ def tile_lstmlayer_v_kernel(
             v = work.tile([P, COLS], F32, bufs=1)
             u = work.tile([P, COLS], F32, bufs=1)
             t["w"] = work.tile([P, COLS], F32, name="w")
-            c0_round = c0_words[:, rnd * PASS_COLS : (rnd + 1) * PASS_COLS]
+            c0_round = c0_loaded[:, :, rnd * H_ROUND : (rnd + 1) * H_ROUND].rearrange("p j w -> p w j")
             nc.vector.tensor_tensor(out=v[:], in0=t["i"][:], in1=t["g"][:], op=ALU.mult)
             nc.vector.tensor_tensor(
-                out=u[:].rearrange("p (s c) -> p s c", s=CHUNK_PASSES),
-                in0=t["f"][:].rearrange("p (s c) -> p s c", s=CHUNK_PASSES),
-                in1=c0_round.unsqueeze(1).to_broadcast([P, CHUNK_PASSES, PASS_COLS]),
+                out=as_words(u[:]),
+                in0=as_words(t["f"][:]),
+                in1=c0_round.unsqueeze(1).to_broadcast([P, CHUNK_PASSES, H_ROUND, PACK]),
                 op=ALU.mult,
             )
-            nc.vector.tensor_tensor(out=t["w"][:], in0=t["o"][:], in1=t["grad"][:], op=ALU.mult)
+            nc.vector.tensor_tensor(
+                out=as_words(t["w"][:]),
+                in0=as_words(t["o"][:]),
+                in1=tokens_innermost(loaded["grad"][:]),
+                op=ALU.mult,
+            )
             pass_cols = [slice(s * PASS_COLS, (s + 1) * PASS_COLS) for s in range(CHUNK_PASSES)]
             if rnd < PLAIN_ROUNDS:
                 t["c"] = []
@@ -214,12 +216,9 @@ def tile_lstmlayer_v_kernel(
                 out=c0_loaded[first_p : first_p + BATCH // PACK], in_=by_partition(c0[:, :])
             )
         load(0, loaded[0], ("f", "o", "grad", "x"))
-        nc.vector.tensor_copy(
-            out=c0_words[:].rearrange("p (w j) -> p w j", j=PACK), in_=c0_loaded[:].rearrange("p j w -> p w j")
-        )
 
         tiles = {0: scalar_front(loaded[0])}
-        vector_front(0, tiles[0])
+        vector_front(0, tiles[0], loaded[0])
         loaded[1] = load_chunk(1)
         tiles[1] = scalar_front(loaded[1])
         scalar_middle(tiles[0], loaded[0])
@@ -229,7 +228,7 @@ def tile_lstmlayer_v_kernel(
                 loaded[n + 2] = load_chunk(n + 2)
                 tiles[n + 2] = scalar_front(loaded[n + 2])
             if n + 1 < CHUNKS:
-                vector_front(n + 1, tiles[n + 1])
+                vector_front(n + 1, tiles[n + 1], loaded[n + 1])
                 scalar_middle(tiles[n + 1], loaded[n + 1])
             vector_back(n, tiles[n])
             if n % ROUND_CHUNKS == 0:

@@ -38,9 +38,10 @@ def tile_lstmlayer_v_kernel(
     tc, x, h0, c0, noise, w_ih, w_hh, b_ih, b_hh, gates, grad_out, out
 ):
     nc = tc.nc
-    gates_rows = gates.flatten_outer_dims()
-    grad_rows = grad_out.flatten_outer_dims()
     x_rows = x.flatten_outer_dims()
+    gates_rows = gates.flatten_outer_dims()
+    dram = {gate: gates_rows[:, q * H : (q + 1) * H] for q, gate in enumerate(GATES)}
+    dram["grad"] = grad_out.flatten_outer_dims()
 
     def by_partition(rows):
         return rows.rearrange("(p j) w -> p j w", j=PACK)
@@ -51,54 +52,64 @@ def tile_lstmlayer_v_kernel(
     def as_words(flat):
         return flat.rearrange("p (s w j) -> p s w j", s=CHUNK_PASSES, j=PACK)
 
+    def pass_tokens(n, s):
+        g = (n % ROUND_CHUNKS) * CHUNK_PASSES + s
+        return slice(g * K_PASS, (g + 1) * K_PASS)
+
     with ExitStack() as stack:
         keep = stack.enter_context(tc.tile_pool(name="keep", bufs=1))
         loads = stack.enter_context(tc.tile_pool(name="loads", bufs=2))
         work = stack.enter_context(tc.tile_pool(name="work", bufs=2))
         psum = stack.enter_context(tc.psum_pool(name="psum", bufs=1))
         stack.enter_context(tc.manual_schedule())
+
         c0_loaded = keep.tile([P, PACK, H], BF16)
         x_codes = keep.tile([P, PASSES, N_IN], U32, align_bytes=64)
         x_scales = keep.tile([P, PASSES, N_IN], U8, align_bytes=64)
         identity = keep.tile([P, P], F32)
         make_identity(nc, identity[:])
 
-        def load(n, loaded, names):
-            rnd, part = divmod(n, ROUND_CHUNKS)
+        tiles = [{} for n in range(CHUNKS)]
+        acc = {}
+
+        def load(n, names):
+            rnd = n // ROUND_CHUNKS
             for name in names:
-                if name == "x":
-                    rows, first, width, dtype = x_rows, 0, N_IN, BF16
-                elif name == "grad":
-                    rows, first, width, dtype = grad_rows, rnd * H_ROUND, H_ROUND, BF16
-                else:
-                    rows, first, width, dtype = gates_rows, GATES.index(name) * H + rnd * H_ROUND, H_ROUND, F32
-                loaded[name] = loads.tile([P, CHUNK_PASSES, PACK, width], dtype, name="loaded_" + name)
+                loaded = loads.tile(
+                    [P, CHUNK_PASSES, PACK, H_ROUND], dram[name].dtype, name="loaded_" + name
+                )
                 for s in range(CHUNK_PASSES):
-                    g = part * CHUNK_PASSES + s
                     nc.sync.dma_start(
-                        out=loaded[name][:, s],
-                        in_=by_partition(rows[g * K_PASS : (g + 1) * K_PASS, first : first + width]),
+                        out=loaded[:, s],
+                        in_=by_partition(
+                            dram[name][pass_tokens(n, s), rnd * H_ROUND : (rnd + 1) * H_ROUND]
+                        ),
                     )
+                tiles[n]["loaded_" + name] = loaded
+
+        def load_x(n):
+            loaded = loads.tile([P, CHUNK_PASSES, PACK, N_IN], BF16, name="loaded_x")
+            for s in range(CHUNK_PASSES):
+                nc.sync.dma_start(out=loaded[:, s], in_=by_partition(x_rows[pass_tokens(n, s), :]))
+            tiles[n]["loaded_x"] = loaded
 
         def load_chunk(n):
-            loaded = {}
-            load(n, loaded, ("i", "g", "f", "o", "grad"))
-            if n < ROUND_CHUNKS:
-                load(n, loaded, ("x",))
-            return loaded
+            load(n, ("i", "g", "f", "o", "grad"))
+            if n - 1 < ROUND_CHUNKS:
+                load_x(n - 1)
 
-        def scalar_front(loaded):
-            t = {}
+        def scalar_front(n):
+            t = tiles[n]
             for gate, func in (("i", ACT.Sigmoid), ("g", ACT.Tanh), ("f", ACT.Sigmoid), ("o", ACT.Sigmoid)):
-                t[gate] = work.tile([P, COLS], F32, name="act_" + gate)
+                t[gate] = work.tile([P, COLS], F32, name="gate_" + gate)
                 nc.scalar.activation(
-                    out=as_words(t[gate][:]), in_=tokens_innermost(loaded[gate][:]), func=func
+                    out=as_words(t[gate][:]), in_=tokens_innermost(t["loaded_" + gate][:]), func=func
                 )
             t["g2"] = work.tile([P, COLS], F32, name="g_squared")
             nc.scalar.activation(out=t["g2"][:], in_=t["g"][:], func=ACT.Square)
-            return t
 
-        def vector_front(n, t, loaded):
+        def vector_front(n):
+            t = tiles[n]
             rnd = n // ROUND_CHUNKS
 
             def minus_one_times(name, in0, in1):
@@ -110,8 +121,8 @@ def tile_lstmlayer_v_kernel(
             v = work.tile([P, COLS], F32, bufs=1)
             u = work.tile([P, COLS], F32, bufs=1)
             t["w"] = work.tile([P, COLS], F32, name="w")
-            c0_round = c0_loaded[:, :, rnd * H_ROUND : (rnd + 1) * H_ROUND].rearrange("p j w -> p w j")
             nc.vector.tensor_tensor(out=v[:], in0=t["i"][:], in1=t["g"][:], op=ALU.mult)
+            c0_round = c0_loaded[:, :, rnd * H_ROUND : (rnd + 1) * H_ROUND].rearrange("p j w -> p w j")
             nc.vector.tensor_tensor(
                 out=as_words(u[:]),
                 in0=as_words(t["f"][:]),
@@ -121,7 +132,7 @@ def tile_lstmlayer_v_kernel(
             nc.vector.tensor_tensor(
                 out=as_words(t["w"][:]),
                 in0=as_words(t["o"][:]),
-                in1=tokens_innermost(loaded["grad"][:]),
+                in1=tokens_innermost(t["loaded_grad"][:]),
                 op=ALU.mult,
             )
             pass_cols = [slice(s * PASS_COLS, (s + 1) * PASS_COLS) for s in range(CHUNK_PASSES)]
@@ -141,7 +152,8 @@ def tile_lstmlayer_v_kernel(
             minus_one_times("ny", t["o"], t["w"])
             minus_one_times("np_g", t["g2"], t["i"])
 
-        def scalar_middle(t, loaded):
+        def scalar_middle(n):
+            t = tiles[n]
             t["ntc"] = work.tile([P, COLS], F32, name="ntc")
             for s in range(CHUNK_PASSES):
                 nc.scalar.activation(
@@ -149,12 +161,12 @@ def tile_lstmlayer_v_kernel(
                 )
             t["tc2"] = work.tile([P, COLS], F32, name="tc_squared")
             nc.scalar.activation(out=t["tc2"][:], in_=t["ntc"][:], func=ACT.Square)
-            if "x" in loaded:
-                t["x"] = work.tile([P, CHUNK_PASSES * N_IN * PACK], BF16, name="x_words", align_bytes=64)
-                nc.scalar.copy(out=as_words(t["x"][:]), in_=tokens_innermost(loaded["x"][:]))
+            if "loaded_x" in t:
+                t["x_words"] = work.tile([P, CHUNK_PASSES * N_IN * PACK], BF16, name="x_words", align_bytes=64)
+                nc.scalar.copy(out=as_words(t["x_words"][:]), in_=tokens_innermost(t["loaded_x"][:]))
 
-        def vector_back(n, t):
-            part = n % ROUND_CHUNKS
+        def vector_back(n):
+            t = tiles[n]
             da = {}
 
             def product(gate, in0, in1):
@@ -180,17 +192,20 @@ def tile_lstmlayer_v_kernel(
             product("g", t["np_g"], ndc)
             quantise("f")
             quantise("g")
-            if "x" in t:
-                chunk_passes = slice(part * CHUNK_PASSES, (part + 1) * CHUNK_PASSES)
+            if "x_words" in t:
+                first = (n % ROUND_CHUNKS) * CHUNK_PASSES
                 nc.vector.quantize_mx(
-                    out=x_codes[:, chunk_passes, :].rearrange("p s n -> p (s n)").bitcast(E4M3_X4),
-                    scales=x_scales[:, chunk_passes, :].rearrange("p s n -> p (s n)"),
-                    in_=t["x"][:],
+                    out=x_codes[:, first : first + CHUNK_PASSES, :].rearrange("p s n -> p (s n)").bitcast(E4M3_X4),
+                    scales=x_scales[:, first : first + CHUNK_PASSES, :].rearrange("p s n -> p (s n)"),
+                    in_=t["x_words"][:],
                 )
 
-        def multiply(n, t, acc):
+        def multiply(n):
+            t = tiles[n]
             rnd, part = divmod(n, ROUND_CHUNKS)
             for gate in ("o", "i", "f", "g"):
+                if part == 0:
+                    acc[gate] = psum.tile([P, N_IN], F32, name="acc_" + gate)
                 for s in range(CHUNK_PASSES):
                     g = part * CHUNK_PASSES + s
                     m_cols = slice(s * H_ROUND, (s + 1) * H_ROUND)
@@ -209,29 +224,29 @@ def tile_lstmlayer_v_kernel(
                     first = GATES.index(gate) * H + rnd * H_ROUND
                     nc.scalar.dma_start(out=out[first : first + H_ROUND, :], in_=result[:])
 
-        loaded = {0: {}}
-        load(0, loaded[0], ("i", "g"))
+        zero = keep.tile([P, 1], F32)
+        half = keep.tile([P, 1], F32)
+        nc.vector.memset(zero[:], 0.0)
+        nc.scalar.activation(out=half[:], in_=zero[:], func=ACT.Sigmoid)
+
+        load(0, ("i", "g", "f"))
         for first_p in range(0, P, BATCH // PACK):
             nc.sync.dma_start(
                 out=c0_loaded[first_p : first_p + BATCH // PACK], in_=by_partition(c0[:, :])
             )
-        load(0, loaded[0], ("f", "o", "grad", "x"))
+        load(0, ("o", "grad"))
 
-        tiles = {0: scalar_front(loaded[0])}
-        vector_front(0, tiles[0], loaded[0])
-        loaded[1] = load_chunk(1)
-        tiles[1] = scalar_front(loaded[1])
-        scalar_middle(tiles[0], loaded[0])
-        acc = {}
+        scalar_front(0)
+        vector_front(0)
+        load_chunk(1)
+        scalar_front(1)
+        scalar_middle(0)
         for n in range(CHUNKS):
             if n + 2 < CHUNKS:
-                loaded[n + 2] = load_chunk(n + 2)
-                tiles[n + 2] = scalar_front(loaded[n + 2])
+                load_chunk(n + 2)
+                scalar_front(n + 2)
             if n + 1 < CHUNKS:
-                vector_front(n + 1, tiles[n + 1], loaded[n + 1])
-                scalar_middle(tiles[n + 1], loaded[n + 1])
-            vector_back(n, tiles[n])
-            if n % ROUND_CHUNKS == 0:
-                for gate in GATES:
-                    acc[gate] = psum.tile([P, N_IN], F32, name="acc_" + gate)
-            multiply(n, tiles[n], acc)
+                vector_front(n + 1)
+                scalar_middle(n + 1)
+            vector_back(n)
+            multiply(n)

@@ -23,15 +23,18 @@ N_IN = 512
 GATES = ("i", "f", "g", "o")
 H_ROUND = P
 ROUNDS = H // H_ROUND
-CHUNK_PASSES = 2
-ROUND_CHUNKS = PASSES // CHUNK_PASSES
-CHUNKS = ROUNDS * ROUND_CHUNKS
-PASS_COLS = H_ROUND * PACK
-COLS = CHUNK_PASSES * PASS_COLS
-PLAIN_ROUNDS = 3
+CHUNKS = ROUNDS * PASSES
+CH = H_ROUND * PACK
+BLOCKS = CH // P
 
 FLOPS = 2 * TOKENS * (4 * H) * N_IN
 BYTES = TOKENS * 4 * H * 4 + 2 * TOKENS * H * 2 + BATCH * H * 2 + 4 * H * N_IN * 4
+
+LOAD_BUFS = {"i": 3, "g": 3, "f": 3, "o": 3, "grad": 4}
+GATE_BUFS = {"i": 5, "f": 5, "o": 5, "g": 3}
+X_QUANTISE_STEPS = (2, 4, 6, 8)
+FIRST_JOB_STEP = 9
+JOBS_A_STEP = 2
 
 
 def tile_lstmlayer_v_kernel(
@@ -47,18 +50,14 @@ def tile_lstmlayer_v_kernel(
         return rows.rearrange("(p j) w -> p j w", j=PACK)
 
     def tokens_innermost(loaded):
-        return loaded.rearrange("p s j w -> p s w j")
+        return loaded.rearrange("p j w -> p w j")
 
     def as_words(flat):
-        return flat.rearrange("p (s w j) -> p s w j", s=CHUNK_PASSES, j=PACK)
-
-    def pass_tokens(n, s):
-        g = (n % ROUND_CHUNKS) * CHUNK_PASSES + s
-        return slice(g * K_PASS, (g + 1) * K_PASS)
+        return flat.rearrange("p (w j) -> p w j", j=PACK)
 
     with ExitStack() as stack:
         keep = stack.enter_context(tc.tile_pool(name="keep", bufs=1))
-        loads = stack.enter_context(tc.tile_pool(name="loads", bufs=2))
+        loads = stack.enter_context(tc.tile_pool(name="loads", bufs=3))
         work = stack.enter_context(tc.tile_pool(name="work", bufs=2))
         psum = stack.enter_context(tc.psum_pool(name="psum", bufs=1))
         stack.enter_context(tc.manual_schedule())
@@ -69,184 +68,192 @@ def tile_lstmlayer_v_kernel(
         identity = keep.tile([P, P], F32)
         make_identity(nc, identity[:])
 
-        tiles = [{} for n in range(CHUNKS)]
-        acc = {}
+        tiles = [{} for k in range(CHUNKS)]
+        codes = {}
+        scales = {}
+        x_tiles = [{} for g in range(PASSES)]
 
-        def load(n, names):
-            rnd = n // ROUND_CHUNKS
+        def load(k, names):
+            rnd, g = divmod(k, PASSES)
             for name in names:
                 loaded = loads.tile(
-                    [P, CHUNK_PASSES, PACK, H_ROUND], dram[name].dtype, name="loaded_" + name
+                    [P, PACK, H_ROUND], dram[name].dtype, name="loaded_" + name, bufs=LOAD_BUFS[name]
                 )
-                for s in range(CHUNK_PASSES):
-                    nc.sync.dma_start(
-                        out=loaded[:, s],
-                        in_=by_partition(
-                            dram[name][pass_tokens(n, s), rnd * H_ROUND : (rnd + 1) * H_ROUND]
-                        ),
-                    )
-                tiles[n]["loaded_" + name] = loaded
+                nc.sync.dma_start(
+                    out=loaded[:],
+                    in_=by_partition(
+                        dram[name][g * K_PASS : (g + 1) * K_PASS, rnd * H_ROUND : (rnd + 1) * H_ROUND]
+                    ),
+                )
+                tiles[k]["loaded_" + name] = loaded
 
-        def load_x(n):
-            loaded = loads.tile([P, CHUNK_PASSES, PACK, N_IN], BF16, name="loaded_x")
-            for s in range(CHUNK_PASSES):
-                nc.sync.dma_start(out=loaded[:, s], in_=by_partition(x_rows[pass_tokens(n, s), :]))
-            tiles[n]["loaded_x"] = loaded
+        def load_x(g):
+            loaded = loads.tile([P, PACK, N_IN], BF16, name="loaded_x", bufs=2)
+            nc.sync.dma_start(out=loaded[:], in_=by_partition(x_rows[g * K_PASS : (g + 1) * K_PASS, :]))
+            x_tiles[g]["loaded"] = loaded
 
-        def load_chunk(n):
-            load(n, ("i", "g", "f", "o", "grad"))
-            if n - 1 < ROUND_CHUNKS:
-                load_x(n - 1)
-
-        def scalar_front(n):
-            t = tiles[n]
+        def scalar_front(k):
+            t = tiles[k]
             for gate, func in (("i", ACT.Sigmoid), ("g", ACT.Tanh), ("f", ACT.Sigmoid), ("o", ACT.Sigmoid)):
-                t[gate] = work.tile([P, COLS], F32, name="gate_" + gate)
+                t[gate] = work.tile([P, CH], F32, name="gate_" + gate, bufs=GATE_BUFS[gate])
                 nc.scalar.activation(
                     out=as_words(t[gate][:]), in_=tokens_innermost(t["loaded_" + gate][:]), func=func
                 )
-            t["g2"] = work.tile([P, COLS], F32, name="g_squared")
+            t["g2"] = work.tile([P, CH], F32, name="g_squared", bufs=GATE_BUFS["i"])
             nc.scalar.activation(out=t["g2"][:], in_=t["g"][:], func=ACT.Square)
 
-        def vector_front(n):
-            t = tiles[n]
-            rnd = n // ROUND_CHUNKS
-
-            def minus_one_times(name, in0, in1):
-                t[name] = work.tile([P, COLS], F32, name=name)
-                nc.vector.scalar_tensor_tensor(
-                    out=t[name][:], in0=in0[:], scalar=1.0, in1=in1[:], op0=ALU.subtract, op1=ALU.mult
-                )
-
-            v = work.tile([P, COLS], F32, bufs=1)
-            u = work.tile([P, COLS], F32, bufs=1)
-            t["w"] = work.tile([P, COLS], F32, name="w")
-            nc.vector.tensor_tensor(out=v[:], in0=t["i"][:], in1=t["g"][:], op=ALU.mult)
-            c0_round = c0_loaded[:, :, rnd * H_ROUND : (rnd + 1) * H_ROUND].rearrange("p j w -> p w j")
-            nc.vector.tensor_tensor(
-                out=as_words(u[:]),
+        def gpsimd_front(k):
+            t = tiles[k]
+            rnd = k // PASSES
+            for name in ("v", "u", "c", "w"):
+                t[name] = work.tile([P, CH], F32, name=name, bufs=4)
+            nc.gpsimd.tensor_tensor(out=t["v"][:], in0=t["i"][:], in1=t["g"][:], op=ALU.mult)
+            nc.gpsimd.tensor_tensor(
+                out=as_words(t["u"][:]),
                 in0=as_words(t["f"][:]),
-                in1=c0_round.unsqueeze(1).to_broadcast([P, CHUNK_PASSES, H_ROUND, PACK]),
+                in1=tokens_innermost(c0_loaded[:, :, rnd * H_ROUND : (rnd + 1) * H_ROUND]),
                 op=ALU.mult,
             )
-            nc.vector.tensor_tensor(
+            nc.gpsimd.tensor_tensor(out=t["c"][:], in0=t["u"][:], in1=t["v"][:], op=ALU.add)
+            nc.gpsimd.tensor_tensor(
                 out=as_words(t["w"][:]),
                 in0=as_words(t["o"][:]),
                 in1=tokens_innermost(t["loaded_grad"][:]),
                 op=ALU.mult,
             )
-            pass_cols = [slice(s * PASS_COLS, (s + 1) * PASS_COLS) for s in range(CHUNK_PASSES)]
-            if rnd < PLAIN_ROUNDS:
-                t["c"] = []
-                for cols in pass_cols:
-                    c_bank = psum.tile([P, PASS_COLS], F32, name="c_bank", bufs=2 * CHUNK_PASSES)
-                    nc.tensor.matmul(out=c_bank[:], lhsT=identity[:], rhs=u[:, cols], start=True, stop=False)
-                    nc.tensor.matmul(out=c_bank[:], lhsT=identity[:], rhs=v[:, cols], start=False, stop=True)
-                    t["c"].append(c_bank[:])
-            else:
-                c = work.tile([P, COLS], F32, bufs=1)
-                nc.vector.tensor_tensor(out=c[:], in0=u[:], in1=v[:], op=ALU.add)
-                t["c"] = [c[:, cols] for cols in pass_cols]
-            minus_one_times("np_i", t["i"], v)
-            minus_one_times("np_f", t["f"], u)
-            minus_one_times("ny", t["o"], t["w"])
-            minus_one_times("np_g", t["g2"], t["i"])
 
-        def scalar_middle(n):
-            t = tiles[n]
-            t["ntc"] = work.tile([P, COLS], F32, name="ntc")
-            for s in range(CHUNK_PASSES):
-                nc.scalar.activation(
-                    out=t["ntc"][:, s * PASS_COLS : (s + 1) * PASS_COLS], in_=t["c"][s], func=ACT.Tanh, scale=-1.0
-                )
-            t["tc2"] = work.tile([P, COLS], F32, name="tc_squared")
+        def turned(source):
+            bank = psum.tile([P, CH], F32, name="stage", bufs=6)
+            for b in range(BLOCKS):
+                cols = slice(b * P, (b + 1) * P)
+                nc.tensor.transpose(out=bank[:, cols], in_=source[:, cols], identity=identity[:])
+            return bank
+
+        def scalar_middle(k):
+            t = tiles[k]
+            c_bank = turned(t["c"])
+            t["ntc"] = work.tile([P, CH], F32, name="ntc", bufs=3)
+            nc.scalar.activation(out=t["ntc"][:], in_=c_bank[:], func=ACT.Tanh, scale=-1.0)
+            t["tc2"] = work.tile([P, CH], F32, name="tc_squared", bufs=2)
             nc.scalar.activation(out=t["tc2"][:], in_=t["ntc"][:], func=ACT.Square)
-            if "loaded_x" in t:
-                t["x_words"] = work.tile([P, CHUNK_PASSES * N_IN * PACK], BF16, name="x_words", align_bytes=64)
-                nc.scalar.copy(out=as_words(t["x_words"][:]), in_=tokens_innermost(t["loaded_x"][:]))
 
-        def vector_back(n):
-            t = tiles[n]
-            da = {}
-
-            def product(gate, in0, in1):
-                da[gate] = work.tile([P, COLS], BF16, name="da_" + gate, bufs=1, align_bytes=64)
-                nc.vector.tensor_tensor(out=da[gate][:], in0=in0[:], in1=in1[:], op=ALU.mult)
-
-            def quantise(gate):
-                t["codes_" + gate] = work.tile([P, COLS // PACK], U32, name="codes_" + gate, align_bytes=64)
-                t["scales_" + gate] = work.tile([P, COLS // PACK], U8, name="scales_" + gate, align_bytes=64)
-                nc.vector.quantize_mx(
-                    out=t["codes_" + gate][:].bitcast(E5M2_X4), scales=t["scales_" + gate][:], in_=da[gate][:]
-                )
-
-            ndc = work.tile([P, COLS], F32, bufs=1)
-            nc.vector.scalar_tensor_tensor(
-                out=ndc[:], in0=t["tc2"][:], scalar=1.0, in1=t["w"][:], op0=ALU.subtract, op1=ALU.mult
+        def x_piece(m):
+            g, half = divmod(m, 2)
+            cols = N_IN // 2
+            if half == 0:
+                x_tiles[g]["words"] = work.tile([P, N_IN * PACK], BF16, name="x_words", bufs=2, align_bytes=64)
+            nc.scalar.copy(
+                out=as_words(x_tiles[g]["words"][:, half * cols * PACK : (half + 1) * cols * PACK]),
+                in_=tokens_innermost(x_tiles[g]["loaded"][:, :, half * cols : (half + 1) * cols]),
             )
-            product("o", t["ny"], t["ntc"])
-            product("i", t["np_i"], ndc)
-            quantise("o")
-            product("f", t["np_f"], ndc)
-            quantise("i")
-            product("g", t["np_g"], ndc)
-            quantise("f")
-            quantise("g")
-            if "x_words" in t:
-                first = (n % ROUND_CHUNKS) * CHUNK_PASSES
-                nc.vector.quantize_mx(
-                    out=x_codes[:, first : first + CHUNK_PASSES, :].rearrange("p s n -> p (s n)").bitcast(E4M3_X4),
-                    scales=x_scales[:, first : first + CHUNK_PASSES, :].rearrange("p s n -> p (s n)"),
-                    in_=t["x_words"][:],
-                )
 
-        def multiply(n):
-            t = tiles[n]
-            rnd, part = divmod(n, ROUND_CHUNKS)
-            for gate in ("o", "i", "f", "g"):
-                if part == 0:
-                    acc[gate] = psum.tile([P, N_IN], F32, name="acc_" + gate)
-                for s in range(CHUNK_PASSES):
-                    g = part * CHUNK_PASSES + s
-                    m_cols = slice(s * H_ROUND, (s + 1) * H_ROUND)
-                    nc.tensor.matmul_mx(
-                        out=acc[gate][:],
-                        lhsT=t["codes_" + gate][:, m_cols].bitcast(E5M2_X4),
-                        lhsT_scale=t["scales_" + gate][:, m_cols],
-                        rhs=x_codes[:, g, :].bitcast(E4M3_X4),
-                        rhs_scale=x_scales[:, g, :],
-                        start=(g == 0),
-                        stop=(g == PASSES - 1),
-                    )
-                if part == ROUND_CHUNKS - 1:
-                    result = work.tile([P, N_IN], F32, name="result", bufs=len(GATES))
-                    nc.scalar.copy(out=result[:], in_=acc[gate][:])
-                    first = GATES.index(gate) * H + rnd * H_ROUND
-                    nc.scalar.dma_start(out=out[first : first + H_ROUND, :], in_=result[:])
+        def x_quantise(g):
+            nc.vector.quantize_mx(
+                out=x_codes[:, g, :].bitcast(E4M3_X4), scales=x_scales[:, g, :], in_=x_tiles[g]["words"][:]
+            )
+
+        def quantise(k):
+            rnd, g = divmod(k, PASSES)
+            if g == 0:
+                codes[rnd] = work.tile([P, PASSES, CH], U32, name="codes", bufs=3, align_bytes=64)
+                scales[rnd] = work.tile([P, PASSES, CH], U8, name="scales", bufs=3, align_bytes=64)
+            nc.vector.quantize_mx(
+                out=codes[rnd][:, g, :].bitcast(E5M2_X4), scales=scales[rnd][:, g, :], in_=tiles[k]["da"][:]
+            )
+
+        def minus_one_times(out_ap, in0, in1):
+            nc.vector.scalar_tensor_tensor(
+                out=out_ap, in0=in0, scalar=1.0, in1=in1, op0=ALU.subtract, op1=ALU.mult
+            )
+
+        def vector_step(k, banks):
+            t = tiles[k]
+            e = {}
+            e_bank = {}
+            for gate in GATES:
+                e[gate] = work.tile([P, CH], F32, name="e_" + gate, bufs=2)
+            ndc = work.tile([P, CH], F32, name="ndc", bufs=2)
+            minus_one_times(ndc[:], t["tc2"][:], banks["w"][:])
+            nc.vector.tensor_tensor(out=e["o"][:], in0=t["ntc"][:], in1=banks["w"][:], op=ALU.mult)
+            e_bank["o"] = turned(e["o"])
+            if k >= 1:
+                quantise(k - 1)
+            nc.vector.tensor_tensor(out=e["i"][:], in0=ndc[:], in1=banks["v"][:], op=ALU.mult)
+            e_bank["i"] = turned(e["i"])
+            nc.vector.tensor_tensor(out=e["f"][:], in0=ndc[:], in1=banks["u"][:], op=ALU.mult)
+            e_bank["f"] = turned(e["f"])
+            if k in X_QUANTISE_STEPS:
+                x_quantise(X_QUANTISE_STEPS.index(k))
+            nc.vector.tensor_tensor(out=e["g"][:], in0=ndc[:], in1=banks["i"][:], op=ALU.mult)
+            e_bank["g"] = turned(e["g"])
+            t["da"] = work.tile([P, len(GATES) * CH], BF16, name="da", bufs=2, align_bytes=64)
+            for gate, factor in (("o", "o"), ("i", "i"), ("f", "f"), ("g", "g2")):
+                q = GATES.index(gate)
+                minus_one_times(t["da"][:, q * CH : (q + 1) * CH], t[factor][:], e_bank[gate][:])
+
+        def multiply(rnd, q):
+            acc = psum.tile([P, N_IN], F32, name="acc", bufs=2)
+            m_cols = slice(q * H_ROUND, (q + 1) * H_ROUND)
+            for g in range(PASSES):
+                nc.tensor.matmul_mx(
+                    out=acc[:],
+                    lhsT=codes[rnd][:, g, m_cols].bitcast(E5M2_X4),
+                    lhsT_scale=scales[rnd][:, g, m_cols],
+                    rhs=x_codes[:, g, :].bitcast(E4M3_X4),
+                    rhs_scale=x_scales[:, g, :],
+                    start=(g == 0),
+                    stop=(g == PASSES - 1),
+                )
+            return acc
+
+        def store(rnd, q, acc):
+            result = work.tile([P, N_IN], F32, name="result", bufs=4)
+            nc.scalar.copy(out=result[:], in_=acc[:])
+            first = q * H + rnd * H_ROUND
+            nc.scalar.dma_start(out=out[first : first + H_ROUND, :], in_=result[:])
 
         zero = keep.tile([P, 1], F32)
-        half = keep.tile([P, 1], F32)
+        half_tile = keep.tile([P, 1], F32)
         nc.vector.memset(zero[:], 0.0)
-        nc.scalar.activation(out=half[:], in_=zero[:], func=ACT.Sigmoid)
+        nc.scalar.activation(out=half_tile[:], in_=zero[:], func=ACT.Sigmoid)
 
-        load(0, ("i", "g", "f"))
-        for first_p in range(0, P, BATCH // PACK):
-            nc.sync.dma_start(
-                out=c0_loaded[first_p : first_p + BATCH // PACK], in_=by_partition(c0[:, :])
-            )
-        load(0, ("o", "grad"))
-
-        scalar_front(0)
-        vector_front(0)
-        load_chunk(1)
-        scalar_front(1)
-        scalar_middle(0)
-        for n in range(CHUNKS):
-            if n + 2 < CHUNKS:
-                load_chunk(n + 2)
-                scalar_front(n + 2)
-            if n + 1 < CHUNKS:
-                vector_front(n + 1)
-                scalar_middle(n + 1)
-            vector_back(n)
-            multiply(n)
+        jobs = []
+        for k in range(-5, CHUNKS):
+            if k + 5 == 0:
+                load(0, ("i", "g", "f"))
+                for first_p in range(0, P, BATCH // PACK):
+                    nc.sync.dma_start(
+                        out=c0_loaded[first_p : first_p + BATCH // PACK], in_=by_partition(c0[:, :])
+                    )
+                load(0, ("o", "grad"))
+            elif k + 5 < CHUNKS:
+                load(k + 5, ("i", "g", "f", "o", "grad"))
+            if k + 2 >= 0 and (k + 2) % 2 == 0 and (k + 2) // 2 < PASSES:
+                load_x((k + 2) // 2)
+            banks = {}
+            if k >= 0:
+                for name in ("w", "v", "u", "i"):
+                    banks[name] = turned(tiles[k][name])
+            if 0 <= k + 1 < CHUNKS:
+                scalar_middle(k + 1)
+            done = []
+            if k >= FIRST_JOB_STEP:
+                for job in jobs[:JOBS_A_STEP]:
+                    done.append((job, multiply(job[0], job[1])))
+                jobs = jobs[JOBS_A_STEP:]
+            if 0 <= k + 3 < CHUNKS:
+                scalar_front(k + 3)
+            if 0 <= k < 2 * PASSES:
+                x_piece(k)
+            for job, acc in done:
+                store(job[0], job[1], acc)
+            if 0 <= k + 2 < CHUNKS:
+                gpsimd_front(k + 2)
+            if k >= 0:
+                vector_step(k, banks)
+                if k >= 1 and (k - 1) % PASSES == PASSES - 1:
+                    jobs.extend([((k - 1) // PASSES, q) for q in (3, 0, 1, 2)])
+        quantise(CHUNKS - 1)
+        jobs.extend([(ROUNDS - 1, q) for q in (3, 0, 1, 2)])
+        for job in jobs:
+            store(job[0], job[1], multiply(job[0], job[1]))

@@ -105,7 +105,7 @@ def tile_lstmlayer_v_kernel(
         def gpsimd_front(k):
             t = tiles[k]
             rnd = k // PASSES
-            for name in ("v", "u", "c", "w"):
+            for name in ("v", "u", "w"):
                 t[name] = work.tile([P, CH], F32, name=name, bufs=4)
             nc.gpsimd.tensor_tensor(out=t["v"][:], in0=t["i"][:], in1=t["g"][:], op=ALU.mult)
             nc.gpsimd.tensor_tensor(
@@ -114,7 +114,6 @@ def tile_lstmlayer_v_kernel(
                 in1=tokens_innermost(c0_loaded[:, :, rnd * H_ROUND : (rnd + 1) * H_ROUND]),
                 op=ALU.mult,
             )
-            nc.gpsimd.tensor_tensor(out=t["c"][:], in0=t["u"][:], in1=t["v"][:], op=ALU.add)
             nc.gpsimd.tensor_tensor(
                 out=as_words(t["w"][:]),
                 in0=as_words(t["o"][:]),
@@ -131,7 +130,15 @@ def tile_lstmlayer_v_kernel(
 
         def scalar_middle(k):
             t = tiles[k]
-            c_bank = turned(t["c"])
+            c_bank = psum.tile([P, CH], F32, name="stage", bufs=6)
+            for b in range(BLOCKS):
+                cols = slice(b * P, (b + 1) * P)
+                nc.tensor.matmul(
+                    out=c_bank[:, cols], lhsT=t["u"][:, cols], rhs=identity[:], is_transpose=True, start=True, stop=False
+                )
+                nc.tensor.matmul(
+                    out=c_bank[:, cols], lhsT=t["v"][:, cols], rhs=identity[:], is_transpose=True, start=False, stop=True
+                )
             t["ntc"] = work.tile([P, CH], F32, name="ntc", bufs=3)
             nc.scalar.activation(out=t["ntc"][:], in_=c_bank[:], func=ACT.Tanh, scale=-1.0)
             t["tc2"] = work.tile([P, CH], F32, name="tc_squared", bufs=2)

@@ -21,6 +21,7 @@ PASSES = TOKENS // K_PASS
 H = 512
 N_IN = 512
 GATES = ("i", "f", "g", "o")
+DA_ORDER = ("f", "i", "g", "o")
 H_ROUND = P
 ROUNDS = H // H_ROUND
 CHUNKS = ROUNDS * PASSES
@@ -30,8 +31,7 @@ BLOCKS = CH // P
 FLOPS = 2 * TOKENS * (4 * H) * N_IN
 BYTES = TOKENS * 4 * H * 4 + 2 * TOKENS * H * 2 + BATCH * H * 2 + 4 * H * N_IN * 4
 
-LOAD_BUFS = {"i": 3, "g": 3, "f": 3, "o": 3, "grad": 4}
-GATE_BUFS = {"i": 5, "f": 5, "o": 5, "g": 3}
+LOAD_BUFS = {"i": 3, "g": 3, "f": 3, "o": 3, "grad": 5}
 X_QUANTISE_STEPS = (2, 4, 6, 8)
 FIRST_JOB_STEP = 9
 JOBS_A_STEP = 2
@@ -55,6 +55,9 @@ def tile_lstmlayer_v_kernel(
     def as_words(flat):
         return flat.rearrange("p (w j) -> p w j", j=PACK)
 
+    def part(n):
+        return slice(n * CH, (n + 1) * CH)
+
     with ExitStack() as stack:
         keep = stack.enter_context(tc.tile_pool(name="keep", bufs=1))
         loads = stack.enter_context(tc.tile_pool(name="loads", bufs=3))
@@ -62,7 +65,6 @@ def tile_lstmlayer_v_kernel(
         psum = stack.enter_context(tc.psum_pool(name="psum", bufs=1))
         stack.enter_context(tc.manual_schedule())
 
-        c0_loaded = keep.tile([P, PACK, H], BF16)
         x_codes = keep.tile([P, PASSES, N_IN], U32, align_bytes=64)
         x_scales = keep.tile([P, PASSES, N_IN], U8, align_bytes=64)
         identity = keep.tile([P, P], F32)
@@ -71,6 +73,7 @@ def tile_lstmlayer_v_kernel(
         tiles = [{} for k in range(CHUNKS)]
         codes = {}
         scales = {}
+        c0_tiles = {}
         x_tiles = [{} for g in range(PASSES)]
 
         def load(k, names):
@@ -87,60 +90,88 @@ def tile_lstmlayer_v_kernel(
                 )
                 tiles[k]["loaded_" + name] = loaded
 
+        def load_c0(rnd):
+            loaded = loads.tile([P, PACK, H_ROUND], BF16, name="loaded_c0", bufs=2)
+            for first_p in range(0, P, BATCH // PACK):
+                nc.sync.dma_start(
+                    out=loaded[first_p : first_p + BATCH // PACK],
+                    in_=by_partition(c0[:, rnd * H_ROUND : (rnd + 1) * H_ROUND]),
+                )
+            c0_tiles[rnd] = loaded
+
         def load_x(g):
             loaded = loads.tile([P, PACK, N_IN], BF16, name="loaded_x", bufs=2)
             nc.sync.dma_start(out=loaded[:], in_=by_partition(x_rows[g * K_PASS : (g + 1) * K_PASS, :]))
             x_tiles[g]["loaded"] = loaded
 
-        def scalar_front(k):
-            t = tiles[k]
-            for gate, func in (("i", ACT.Sigmoid), ("g", ACT.Tanh), ("f", ACT.Sigmoid), ("o", ACT.Sigmoid)):
-                t[gate] = work.tile([P, CH], F32, name="gate_" + gate, bufs=GATE_BUFS[gate])
-                nc.scalar.activation(
-                    out=as_words(t[gate][:]), in_=tokens_innermost(t["loaded_" + gate][:]), func=func
-                )
-            t["g2"] = work.tile([P, CH], F32, name="g_squared", bufs=GATE_BUFS["i"])
-            nc.scalar.activation(out=t["g2"][:], in_=t["g"][:], func=ACT.Square)
+        def activate(k, out_ap, gate, func):
+            nc.scalar.activation(
+                out=as_words(out_ap), in_=tokens_innermost(tiles[k]["loaded_" + gate][:]), func=func
+            )
 
-        def gpsimd_front(k):
+        def gates_first(k):
             t = tiles[k]
-            rnd = k // PASSES
-            for name in ("v", "u", "w"):
-                t[name] = work.tile([P, CH], F32, name=name, bufs=4)
-            nc.gpsimd.tensor_tensor(out=t["v"][:], in0=t["i"][:], in1=t["g"][:], op=ALU.mult)
-            nc.gpsimd.tensor_tensor(
-                out=as_words(t["u"][:]),
-                in0=as_words(t["f"][:]),
-                in1=tokens_innermost(c0_loaded[:, :, rnd * H_ROUND : (rnd + 1) * H_ROUND]),
+            t["fiw"] = work.tile([P, 3 * CH], F32, name="fiw", bufs=4)
+            t["go"] = work.tile([P, 2 * CH], F32, name="go", bufs=4)
+            t["g"] = work.tile([P, CH], F32, name="gate_g", bufs=3)
+            activate(k, t["fiw"][:, part(1)], "i", ACT.Sigmoid)
+            activate(k, t["g"][:], "g", ACT.Tanh)
+
+        def gates_second(k):
+            t = tiles[k]
+            activate(k, t["fiw"][:, part(0)], "f", ACT.Sigmoid)
+            activate(k, t["go"][:, part(1)], "o", ACT.Sigmoid)
+
+        def gates_third(k):
+            t = tiles[k]
+            nc.scalar.activation(out=t["go"][:, part(0)], in_=t["g"][:], func=ACT.Square)
+
+        def uv(k, engine):
+            t = tiles[k]
+            t["uv"] = work.tile([P, 2 * CH], F32, name="uv", bufs=2)
+            engine.tensor_tensor(out=t["uv"][:, part(1)], in0=t["fiw"][:, part(1)], in1=t["g"][:], op=ALU.mult)
+            engine.tensor_tensor(
+                out=as_words(t["uv"][:, part(0)]),
+                in0=as_words(t["fiw"][:, part(0)]),
+                in1=tokens_innermost(c0_tiles[k // PASSES][:]),
                 op=ALU.mult,
             )
-            nc.gpsimd.tensor_tensor(
-                out=as_words(t["w"][:]),
-                in0=as_words(t["o"][:]),
+
+        def make_w(k):
+            t = tiles[k]
+            nc.vector.tensor_tensor(
+                out=as_words(t["fiw"][:, part(2)]),
+                in0=as_words(t["go"][:, part(1)]),
                 in1=tokens_innermost(t["loaded_grad"][:]),
                 op=ALU.mult,
             )
 
-        def turned(source):
-            bank = psum.tile([P, CH], F32, name="stage", bufs=6)
+        def turned(source, name, bufs):
+            bank = psum.tile([P, CH], F32, name=name, bufs=bufs)
             for b in range(BLOCKS):
                 cols = slice(b * P, (b + 1) * P)
                 nc.tensor.transpose(out=bank[:, cols], in_=source[:, cols], identity=identity[:])
             return bank
 
-        def scalar_middle(k):
+        def c_bank(k):
             t = tiles[k]
-            c_bank = psum.tile([P, CH], F32, name="stage", bufs=6)
+            t["c"] = psum.tile([P, CH], F32, name="c_bank", bufs=2)
             for b in range(BLOCKS):
                 cols = slice(b * P, (b + 1) * P)
-                nc.tensor.matmul(
-                    out=c_bank[:, cols], lhsT=t["u"][:, cols], rhs=identity[:], is_transpose=True, start=True, stop=False
-                )
-                nc.tensor.matmul(
-                    out=c_bank[:, cols], lhsT=t["v"][:, cols], rhs=identity[:], is_transpose=True, start=False, stop=True
-                )
-            t["ntc"] = work.tile([P, CH], F32, name="ntc", bufs=3)
-            nc.scalar.activation(out=t["ntc"][:], in_=c_bank[:], func=ACT.Tanh, scale=-1.0)
+                for n in range(2):
+                    nc.tensor.matmul(
+                        out=t["c"][:, cols],
+                        lhsT=t["uv"][:, n * CH + b * P : n * CH + (b + 1) * P],
+                        rhs=identity[:],
+                        is_transpose=True,
+                        start=(n == 0),
+                        stop=(n == 1),
+                    )
+
+        def tanh_c(k):
+            t = tiles[k]
+            t["ntc"] = work.tile([P, CH], F32, name="ntc", bufs=2)
+            nc.scalar.activation(out=t["ntc"][:], in_=t["c"][:], func=ACT.Tanh, scale=-1.0)
             t["tc2"] = work.tile([P, CH], F32, name="tc_squared", bufs=2)
             nc.scalar.activation(out=t["tc2"][:], in_=t["ntc"][:], func=ACT.Square)
 
@@ -173,30 +204,32 @@ def tile_lstmlayer_v_kernel(
                 out=out_ap, in0=in0, scalar=1.0, in1=in1, op0=ALU.subtract, op1=ALU.mult
             )
 
-        def vector_step(k, banks):
+        def factors_fi(k):
             t = tiles[k]
-            e = {}
-            e_bank = {}
-            for gate in GATES:
-                e[gate] = work.tile([P, CH], F32, name="e_" + gate, bufs=2)
-            ndc = work.tile([P, CH], F32, name="ndc", bufs=2)
-            minus_one_times(ndc[:], t["tc2"][:], banks["w"][:])
-            nc.vector.tensor_tensor(out=e["o"][:], in0=t["ntc"][:], in1=banks["w"][:], op=ALU.mult)
-            e_bank["o"] = turned(e["o"])
-            if k >= 1:
-                quantise(k - 1)
-            nc.vector.tensor_tensor(out=e["i"][:], in0=ndc[:], in1=banks["v"][:], op=ALU.mult)
-            e_bank["i"] = turned(e["i"])
-            nc.vector.tensor_tensor(out=e["f"][:], in0=ndc[:], in1=banks["u"][:], op=ALU.mult)
-            e_bank["f"] = turned(e["f"])
-            if k in X_QUANTISE_STEPS:
-                x_quantise(X_QUANTISE_STEPS.index(k))
-            nc.vector.tensor_tensor(out=e["g"][:], in0=ndc[:], in1=banks["i"][:], op=ALU.mult)
-            e_bank["g"] = turned(e["g"])
-            t["da"] = work.tile([P, len(GATES) * CH], BF16, name="da", bufs=2, align_bytes=64)
-            for gate, factor in (("o", "o"), ("i", "i"), ("f", "f"), ("g", "g2")):
-                q = GATES.index(gate)
-                minus_one_times(t["da"][:, q * CH : (q + 1) * CH], t[factor][:], e_bank[gate][:])
+            t["p"] = work.tile([P, 4 * CH], F32, name="factors", bufs=2)
+            minus_one_times(t["p"][:, 0 : 2 * CH], t["fiw"][:, 0 : 2 * CH], t["uv"][:])
+
+        def factors_go(k):
+            t = tiles[k]
+            minus_one_times(t["p"][:, 2 * CH : 4 * CH], t["go"][:], t["fiw"][:, CH : 3 * CH])
+
+        def turned_dc(k):
+            t = tiles[k]
+            t["ndc"] = work.tile([P, CH], F32, name="ndc", bufs=2)
+            minus_one_times(t["ndc"][:], t["tc2"][:], t["w_bank"][:])
+
+        def finish(k):
+            t = tiles[k]
+            t["da"] = work.tile([P, 4 * CH], BF16, name="da", bufs=2, align_bytes=64)
+            nc.vector.tensor_tensor(
+                out=t["da"][:, part(3)], in0=t["p"][:, part(3)], in1=t["ntc_bank"][:], op=ALU.mult
+            )
+            nc.vector.tensor_tensor(
+                out=t["da"][:, 0 : 3 * CH].rearrange("p (n w) -> p n w", n=3),
+                in0=t["p"][:, 0 : 3 * CH].rearrange("p (n w) -> p n w", n=3),
+                in1=t["ndc_bank"][:].unsqueeze(1).to_broadcast([P, 3, CH]),
+                op=ALU.mult,
+            )
 
         def multiply(rnd, q):
             acc = psum.tile([P, N_IN], F32, name="acc", bufs=2)
@@ -216,7 +249,7 @@ def tile_lstmlayer_v_kernel(
         def store(rnd, q, acc):
             result = work.tile([P, N_IN], F32, name="result", bufs=4)
             nc.scalar.copy(out=result[:], in_=acc[:])
-            first = q * H + rnd * H_ROUND
+            first = GATES.index(DA_ORDER[q]) * H + rnd * H_ROUND
             nc.scalar.dma_start(out=out[first : first + H_ROUND, :], in_=result[:])
 
         zero = keep.tile([P, 1], F32)
@@ -224,43 +257,84 @@ def tile_lstmlayer_v_kernel(
         nc.vector.memset(zero[:], 0.0)
         nc.scalar.activation(out=half_tile[:], in_=zero[:], func=ACT.Sigmoid)
 
+        load(0, ("i", "g", "f"))
+        load_c0(0)
+        load(0, ("o", "grad"))
+        for k in range(1, 5):
+            load(k, ("i", "g", "f", "o", "grad"))
+            if k == 2:
+                load_c0(1)
+                load_x(0)
+        gates_first(0)
+        gates_second(0)
+        uv(0, nc.vector)
+        make_w(0)
+        gates_first(1)
+        c_bank(0)
+        tiles[0]["w_bank"] = turned(tiles[0]["fiw"][:, part(2)], "w_bank", 1)
+        tanh_c(0)
+        tiles[0]["ntc_bank"] = turned(tiles[0]["ntc"], "ntc_bank", 2)
+        factors_fi(0)
+        gates_second(1)
+        gates_third(0)
+        gates_third(1)
+        uv(1, nc.gpsimd)
+        gates_first(2)
+        gates_second(2)
+        gates_third(2)
+        turned_dc(0)
+        tiles[0]["ndc_bank"] = turned(tiles[0]["ndc"], "ndc_bank", 1)
+
         jobs = []
-        for k in range(-5, CHUNKS):
-            if k + 5 == 0:
-                load(0, ("i", "g", "f"))
-                for first_p in range(0, P, BATCH // PACK):
-                    nc.sync.dma_start(
-                        out=c0_loaded[first_p : first_p + BATCH // PACK], in_=by_partition(c0[:, :])
-                    )
-                load(0, ("o", "grad"))
-            elif k + 5 < CHUNKS:
+        for k in range(CHUNKS):
+            if k + 5 < CHUNKS:
                 load(k + 5, ("i", "g", "f", "o", "grad"))
-            if k + 2 >= 0 and (k + 2) % 2 == 0 and (k + 2) // 2 < PASSES:
+                if (k + 5) % PASSES == 2 and (k + 5) // PASSES + 1 < ROUNDS:
+                    load_c0((k + 5) // PASSES + 1)
+            if (k + 2) % 2 == 0 and (k + 2) // 2 < PASSES:
                 load_x((k + 2) // 2)
-            banks = {}
-            if k >= 0:
-                for name in ("w", "v", "u", "i"):
-                    banks[name] = turned(tiles[k][name])
-            if 0 <= k + 1 < CHUNKS:
-                scalar_middle(k + 1)
+            if k >= 1:
+                quantise(k - 1)
+                if (k - 1) % PASSES == PASSES - 1:
+                    jobs.extend([((k - 1) // PASSES, q) for q in range(4)])
+            if k in X_QUANTISE_STEPS:
+                x_quantise(X_QUANTISE_STEPS.index(k))
+            if k + 1 < CHUNKS:
+                make_w(k + 1)
+                c_bank(k + 1)
+                tiles[k + 1]["w_bank"] = turned(tiles[k + 1]["fiw"][:, part(2)], "w_bank", 1)
+            if k + 3 < CHUNKS:
+                gates_first(k + 3)
+            if k + 1 < CHUNKS:
+                tanh_c(k + 1)
             done = []
             if k >= FIRST_JOB_STEP:
                 for job in jobs[:JOBS_A_STEP]:
                     done.append((job, multiply(job[0], job[1])))
                 jobs = jobs[JOBS_A_STEP:]
-            if 0 <= k + 3 < CHUNKS:
-                scalar_front(k + 3)
-            if 0 <= k < 2 * PASSES:
+            if k + 1 < CHUNKS:
+                tiles[k + 1]["ntc_bank"] = turned(tiles[k + 1]["ntc"], "ntc_bank", 2)
+            if k + 3 < CHUNKS:
+                gates_second(k + 3)
+                gates_third(k + 3)
+            if k < 2 * PASSES:
                 x_piece(k)
             for job, acc in done:
                 store(job[0], job[1], acc)
-            if 0 <= k + 2 < CHUNKS:
-                gpsimd_front(k + 2)
-            if k >= 0:
-                vector_step(k, banks)
-                if k >= 1 and (k - 1) % PASSES == PASSES - 1:
-                    jobs.extend([((k - 1) // PASSES, q) for q in (3, 0, 1, 2)])
+            if k == 0:
+                factors_go(k)
+            else:
+                t = tiles[k]
+                t["p"] = work.tile([P, 4 * CH], F32, name="factors", bufs=2)
+                factors_go(k)
+                minus_one_times(t["p"][:, 0 : 2 * CH], t["fiw"][:, 0 : 2 * CH], t["uv"][:])
+            finish(k)
+            if k + 1 < CHUNKS:
+                turned_dc(k + 1)
+                tiles[k + 1]["ndc_bank"] = turned(tiles[k + 1]["ndc"], "ndc_bank", 1)
+            if k + 2 < CHUNKS:
+                uv(k + 2, nc.gpsimd)
         quantise(CHUNKS - 1)
-        jobs.extend([(ROUNDS - 1, q) for q in (3, 0, 1, 2)])
+        jobs.extend([(ROUNDS - 1, q) for q in range(4)])
         for job in jobs:
             store(job[0], job[1], multiply(job[0], job[1]))

@@ -74,6 +74,7 @@ def tile_lstmlayer_v_kernel(
         codes = {}
         scales = {}
         c0_tiles = {}
+        c0_words = {}
         x_tiles = [{} for g in range(PASSES)]
 
         def load(k, names):
@@ -98,6 +99,11 @@ def tile_lstmlayer_v_kernel(
                     in_=by_partition(c0[:, rnd * H_ROUND : (rnd + 1) * H_ROUND]),
                 )
             c0_tiles[rnd] = loaded
+
+        def regroup_c0(rnd):
+            words = work.tile([P, CH], BF16, name="c0_words", bufs=2)
+            nc.vector.tensor_copy(out=as_words(words[:]), in_=tokens_innermost(c0_tiles[rnd][:]))
+            c0_words[rnd] = words
 
         def load_x(g):
             loaded = loads.tile([P, PACK, N_IN], BF16, name="loaded_x", bufs=2)
@@ -131,10 +137,7 @@ def tile_lstmlayer_v_kernel(
             t["uv"] = work.tile([P, 2 * CH], F32, name="uv", bufs=2)
             engine.tensor_tensor(out=t["uv"][:, part(1)], in0=t["fiw"][:, part(1)], in1=t["g"][:], op=ALU.mult)
             engine.tensor_tensor(
-                out=as_words(t["uv"][:, part(0)]),
-                in0=as_words(t["fiw"][:, part(0)]),
-                in1=tokens_innermost(c0_tiles[k // PASSES][:]),
-                op=ALU.mult,
+                out=t["uv"][:, part(0)], in0=t["fiw"][:, part(0)], in1=c0_words[k // PASSES][:], op=ALU.mult
             )
 
         def make_w(k):
@@ -204,9 +207,11 @@ def tile_lstmlayer_v_kernel(
                 out=out_ap, in0=in0, scalar=1.0, in1=in1, op0=ALU.subtract, op1=ALU.mult
             )
 
+        def factors(k):
+            tiles[k]["p"] = work.tile([P, 4 * CH], F32, name="factors", bufs=2)
+
         def factors_fi(k):
             t = tiles[k]
-            t["p"] = work.tile([P, 4 * CH], F32, name="factors", bufs=2)
             minus_one_times(t["p"][:, 0 : 2 * CH], t["fiw"][:, 0 : 2 * CH], t["uv"][:])
 
         def factors_go(k):
@@ -267,6 +272,7 @@ def tile_lstmlayer_v_kernel(
                 load_x(0)
         gates_first(0)
         gates_second(0)
+        regroup_c0(0)
         uv(0, nc.vector)
         make_w(0)
         gates_first(1)
@@ -274,6 +280,7 @@ def tile_lstmlayer_v_kernel(
         tiles[0]["w_bank"] = turned(tiles[0]["fiw"][:, part(2)], "w_bank", 1)
         tanh_c(0)
         tiles[0]["ntc_bank"] = turned(tiles[0]["ntc"], "ntc_bank", 2)
+        factors(0)
         factors_fi(0)
         gates_second(1)
         gates_third(0)
@@ -299,10 +306,10 @@ def tile_lstmlayer_v_kernel(
                     jobs.extend([((k - 1) // PASSES, q) for q in range(4)])
             if k in X_QUANTISE_STEPS:
                 x_quantise(X_QUANTISE_STEPS.index(k))
+            if (k + 3) % PASSES == 0 and k + 3 < CHUNKS:
+                regroup_c0((k + 3) // PASSES)
             if k + 1 < CHUNKS:
-                make_w(k + 1)
                 c_bank(k + 1)
-                tiles[k + 1]["w_bank"] = turned(tiles[k + 1]["fiw"][:, part(2)], "w_bank", 1)
             if k + 3 < CHUNKS:
                 gates_first(k + 3)
             if k + 1 < CHUNKS:
@@ -312,8 +319,6 @@ def tile_lstmlayer_v_kernel(
                 for job in jobs[:JOBS_A_STEP]:
                     done.append((job, multiply(job[0], job[1])))
                 jobs = jobs[JOBS_A_STEP:]
-            if k + 1 < CHUNKS:
-                tiles[k + 1]["ntc_bank"] = turned(tiles[k + 1]["ntc"], "ntc_bank", 2)
             if k + 3 < CHUNKS:
                 gates_second(k + 3)
                 gates_third(k + 3)
@@ -321,13 +326,16 @@ def tile_lstmlayer_v_kernel(
                 x_piece(k)
             for job, acc in done:
                 store(job[0], job[1], acc)
-            if k == 0:
+            if k > 0:
+                factors(k)
                 factors_go(k)
+                factors_fi(k)
             else:
-                t = tiles[k]
-                t["p"] = work.tile([P, 4 * CH], F32, name="factors", bufs=2)
                 factors_go(k)
-                minus_one_times(t["p"][:, 0 : 2 * CH], t["fiw"][:, 0 : 2 * CH], t["uv"][:])
+            if k + 1 < CHUNKS:
+                make_w(k + 1)
+                tiles[k + 1]["w_bank"] = turned(tiles[k + 1]["fiw"][:, part(2)], "w_bank", 1)
+                tiles[k + 1]["ntc_bank"] = turned(tiles[k + 1]["ntc"], "ntc_bank", 2)
             finish(k)
             if k + 1 < CHUNKS:
                 turned_dc(k + 1)

@@ -32,7 +32,7 @@ FLOPS = 2 * TOKENS * (4 * H) * N_IN
 BYTES = TOKENS * 4 * H * 4 + 2 * TOKENS * H * 2 + BATCH * H * 2 + 4 * H * N_IN * 4
 
 LOAD_BUFS = {"i": 3, "g": 3, "f": 3, "o": 3, "grad": 5}
-X_QUANTISE_STEPS = (2, 4, 6, 8)
+X_QUANTISE_STEPS = (3, 5, 7, 9)
 FIRST_JOB_STEP = 9
 JOBS_A_STEP = 2
 
@@ -115,27 +115,33 @@ def tile_lstmlayer_v_kernel(
                 out=as_words(out_ap), in_=tokens_innermost(tiles[k]["loaded_" + gate][:]), func=func
             )
 
-        def gates_first(k):
+        def start_chunk(k):
             t = tiles[k]
             t["fiw"] = work.tile([P, 3 * CH], F32, name="fiw", bufs=4)
             t["go"] = work.tile([P, 2 * CH], F32, name="go", bufs=4)
             t["g"] = work.tile([P, CH], F32, name="gate_g", bufs=3)
-            activate(k, t["fiw"][:, part(1)], "i", ACT.Sigmoid)
-            activate(k, t["g"][:], "g", ACT.Tanh)
 
-        def gates_second(k):
-            t = tiles[k]
-            activate(k, t["fiw"][:, part(0)], "f", ACT.Sigmoid)
-            activate(k, t["go"][:, part(1)], "o", ACT.Sigmoid)
+        def gate_ig(k):
+            start_chunk(k)
+            activate(k, tiles[k]["fiw"][:, part(1)], "i", ACT.Sigmoid)
+            activate(k, tiles[k]["g"][:], "g", ACT.Tanh)
 
-        def gates_third(k):
-            t = tiles[k]
-            nc.scalar.activation(out=t["go"][:, part(0)], in_=t["g"][:], func=ACT.Square)
+        def gate_f(k):
+            activate(k, tiles[k]["fiw"][:, part(0)], "f", ACT.Sigmoid)
 
-        def uv(k, engine):
+        def gate_o(k):
+            activate(k, tiles[k]["go"][:, part(1)], "o", ACT.Sigmoid)
+
+        def square_g(k):
+            nc.scalar.activation(out=tiles[k]["go"][:, part(0)], in_=tiles[k]["g"][:], func=ACT.Square)
+
+        def product_v(k, engine):
             t = tiles[k]
             t["uv"] = work.tile([P, 2 * CH], F32, name="uv", bufs=2)
             engine.tensor_tensor(out=t["uv"][:, part(1)], in0=t["fiw"][:, part(1)], in1=t["g"][:], op=ALU.mult)
+
+        def product_u(k, engine):
+            t = tiles[k]
             engine.tensor_tensor(
                 out=t["uv"][:, part(0)], in0=t["fiw"][:, part(0)], in1=c0_words[k // PASSES][:], op=ALU.mult
             )
@@ -155,6 +161,15 @@ def tile_lstmlayer_v_kernel(
                 cols = slice(b * P, (b + 1) * P)
                 nc.tensor.transpose(out=bank[:, cols], in_=source[:, cols], identity=identity[:])
             return bank
+
+        def turn_w(k):
+            tiles[k]["w_bank"] = turned(tiles[k]["fiw"][:, part(2)], "w_bank", 1)
+
+        def turn_back_ntc(k):
+            tiles[k]["ntc_bank"] = turned(tiles[k]["ntc"], "ntc_bank", 2)
+
+        def turn_back_ndc(k):
+            tiles[k]["ndc_bank"] = turned(tiles[k]["ndc"], "ndc_bank", 1)
 
         def c_bank(k):
             t = tiles[k]
@@ -223,9 +238,24 @@ def tile_lstmlayer_v_kernel(
             t["ndc"] = work.tile([P, CH], F32, name="ndc", bufs=2)
             minus_one_times(t["ndc"][:], t["tc2"][:], t["w_bank"][:])
 
+        def finish_gate(k, q, bank):
+            t = tiles[k]
+            nc.vector.tensor_tensor(out=t["da"][:, part(q)], in0=t["p"][:, part(q)], in1=t[bank][:], op=ALU.mult)
+
+        def quantise_gate(k, q):
+            rnd, g = divmod(k, PASSES)
+            nc.vector.quantize_mx(
+                out=codes[rnd][:, g, q * H_ROUND : (q + 1) * H_ROUND].bitcast(E5M2_X4),
+                scales=scales[rnd][:, g, q * H_ROUND : (q + 1) * H_ROUND],
+                in_=tiles[k]["da"][:, part(q)],
+            )
+
+        def new_da(k):
+            tiles[k]["da"] = work.tile([P, 4 * CH], BF16, name="da", bufs=2, align_bytes=64)
+
         def finish(k):
             t = tiles[k]
-            t["da"] = work.tile([P, 4 * CH], BF16, name="da", bufs=2, align_bytes=64)
+            new_da(k)
             nc.vector.tensor_tensor(
                 out=t["da"][:, part(3)], in0=t["p"][:, part(3)], in1=t["ntc_bank"][:], op=ALU.mult
             )
@@ -236,10 +266,9 @@ def tile_lstmlayer_v_kernel(
                 op=ALU.mult,
             )
 
-        def multiply(rnd, q):
-            acc = psum.tile([P, N_IN], F32, name="acc", bufs=2)
+        def add_passes(acc, rnd, q, passes):
             m_cols = slice(q * H_ROUND, (q + 1) * H_ROUND)
-            for g in range(PASSES):
+            for g in passes:
                 nc.tensor.matmul_mx(
                     out=acc[:],
                     lhsT=codes[rnd][:, g, m_cols].bitcast(E5M2_X4),
@@ -249,13 +278,17 @@ def tile_lstmlayer_v_kernel(
                     start=(g == 0),
                     stop=(g == PASSES - 1),
                 )
+
+        def multiply(rnd, q):
+            acc = psum.tile([P, N_IN], F32, name="acc", bufs=2)
+            add_passes(acc, rnd, q, range(PASSES))
             return acc
 
-        def store(rnd, q, acc):
+        def store(rnd, q, acc, copy, dma_start):
             result = work.tile([P, N_IN], F32, name="result", bufs=4)
-            nc.scalar.copy(out=result[:], in_=acc[:])
+            copy(out=result[:], in_=acc[:])
             first = GATES.index(DA_ORDER[q]) * H + rnd * H_ROUND
-            nc.scalar.dma_start(out=out[first : first + H_ROUND, :], in_=result[:])
+            dma_start(out=out[first : first + H_ROUND, :], in_=result[:])
 
         zero = keep.tile([P, 1], F32)
         half_tile = keep.tile([P, 1], F32)
@@ -264,85 +297,119 @@ def tile_lstmlayer_v_kernel(
 
         load(0, ("i", "g", "f"))
         load_c0(0)
+        load(1, ("i", "g"))
         load(0, ("o", "grad"))
-        for k in range(1, 5):
+        load(1, ("f", "o", "grad"))
+        load(2, ("i", "g", "f", "o", "grad"))
+        load_c0(1)
+        load_x(0)
+        for k in range(3, 6):
             load(k, ("i", "g", "f", "o", "grad"))
-            if k == 2:
-                load_c0(1)
-                load_x(0)
-        gates_first(0)
-        gates_second(0)
+        gate_ig(0)
+        product_v(0, nc.vector)
         regroup_c0(0)
-        uv(0, nc.vector)
-        make_w(0)
-        gates_first(1)
+        gate_f(0)
+        product_u(0, nc.vector)
         c_bank(0)
-        tiles[0]["w_bank"] = turned(tiles[0]["fiw"][:, part(2)], "w_bank", 1)
-        tanh_c(0)
-        tiles[0]["ntc_bank"] = turned(tiles[0]["ntc"], "ntc_bank", 2)
+        gate_ig(1)
         factors(0)
         factors_fi(0)
-        gates_second(1)
-        gates_third(0)
-        gates_third(1)
-        uv(1, nc.gpsimd)
-        gates_first(2)
-        gates_second(2)
-        gates_third(2)
+        gate_o(0)
+        make_w(0)
+        turn_w(0)
+        gate_f(1)
+        tanh_c(0)
+        product_v(1, nc.vector)
+        product_u(1, nc.vector)
+        c_bank(1)
+        turn_back_ntc(0)
+        square_g(0)
+        gate_o(1)
         turned_dc(0)
-        tiles[0]["ndc_bank"] = turned(tiles[0]["ndc"], "ndc_bank", 1)
+        turn_back_ndc(0)
+        factors_go(0)
+        make_w(1)
+        turn_w(1)
+        tanh_c(1)
+        turn_back_ntc(1)
+        square_g(1)
+        gate_ig(2)
+        gate_f(2)
+        gate_o(2)
+        square_g(2)
+        gate_ig(3)
+        finish(0)
+        turned_dc(1)
+        turn_back_ndc(1)
+        product_v(2, nc.gpsimd)
+        product_u(2, nc.gpsimd)
 
         jobs = []
-        for k in range(CHUNKS):
+        for k in range(1, CHUNKS):
             if k + 5 < CHUNKS:
                 load(k + 5, ("i", "g", "f", "o", "grad"))
                 if (k + 5) % PASSES == 2 and (k + 5) // PASSES + 1 < ROUNDS:
                     load_c0((k + 5) // PASSES + 1)
-            if (k + 2) % 2 == 0 and (k + 2) // 2 < PASSES:
-                load_x((k + 2) // 2)
-            if k >= 1:
-                quantise(k - 1)
-                if (k - 1) % PASSES == PASSES - 1:
-                    jobs.extend([((k - 1) // PASSES, q) for q in range(4)])
-            if k in X_QUANTISE_STEPS:
-                x_quantise(X_QUANTISE_STEPS.index(k))
+            if (k + 1) % 2 == 0 and (k + 1) // 2 < PASSES:
+                load_x((k + 1) // 2)
+            quantise(k - 1)
+            if (k - 1) % PASSES == PASSES - 1:
+                jobs.extend([((k - 1) // PASSES, q) for q in range(4)])
             if (k + 3) % PASSES == 0 and k + 3 < CHUNKS:
                 regroup_c0((k + 3) // PASSES)
+            if k + 2 < CHUNKS:
+                gate_f(k + 2)
+                gate_o(k + 2)
             if k + 1 < CHUNKS:
                 c_bank(k + 1)
-            if k + 3 < CHUNKS:
-                gates_first(k + 3)
-            if k + 1 < CHUNKS:
                 tanh_c(k + 1)
-            done = []
-            if k >= FIRST_JOB_STEP:
-                for job in jobs[:JOBS_A_STEP]:
-                    done.append((job, multiply(job[0], job[1])))
-                jobs = jobs[JOBS_A_STEP:]
+            if k + 2 < CHUNKS:
+                square_g(k + 2)
             if k + 3 < CHUNKS:
-                gates_second(k + 3)
-                gates_third(k + 3)
-            if k < 2 * PASSES:
-                x_piece(k)
-            for job, acc in done:
-                store(job[0], job[1], acc)
-            if k > 0:
-                factors(k)
-                factors_go(k)
-                factors_fi(k)
-            else:
-                factors_go(k)
+                gate_ig(k + 3)
+            if k - 1 < 2 * PASSES:
+                x_piece(k - 1)
+            factors(k)
+            factors_go(k)
+            if k in X_QUANTISE_STEPS:
+                x_quantise(X_QUANTISE_STEPS.index(k))
+            factors_fi(k)
             if k + 1 < CHUNKS:
                 make_w(k + 1)
-                tiles[k + 1]["w_bank"] = turned(tiles[k + 1]["fiw"][:, part(2)], "w_bank", 1)
-                tiles[k + 1]["ntc_bank"] = turned(tiles[k + 1]["ntc"], "ntc_bank", 2)
-            finish(k)
+                turn_w(k + 1)
+                turn_back_ntc(k + 1)
+            if k >= FIRST_JOB_STEP:
+                for job in jobs[:JOBS_A_STEP]:
+                    store(job[0], job[1], multiply(job[0], job[1]), nc.scalar.copy, nc.scalar.dma_start)
+                jobs = jobs[JOBS_A_STEP:]
             if k + 1 < CHUNKS:
+                finish(k)
                 turned_dc(k + 1)
-                tiles[k + 1]["ndc_bank"] = turned(tiles[k + 1]["ndc"], "ndc_bank", 1)
+                turn_back_ndc(k + 1)
             if k + 2 < CHUNKS:
-                uv(k + 2, nc.gpsimd)
-        quantise(CHUNKS - 1)
-        jobs.extend([(ROUNDS - 1, q) for q in range(4)])
-        for job in jobs:
-            store(job[0], job[1], multiply(job[0], job[1]))
+                product_v(k + 2, nc.gpsimd)
+                product_u(k + 2, nc.gpsimd)
+
+        last = CHUNKS - 1
+        accs = {}
+        for q in (3, 0):
+            accs[q] = psum.tile([P, N_IN], F32, name="acc", bufs=2)
+        for q in (1, 2):
+            accs[q] = psum.tile([P, N_IN], F32, name="c_bank", bufs=2)
+        for q in (3, 0, 1, 2):
+            add_passes(accs[q], ROUNDS - 1, q, range(PASSES - 1))
+        new_da(last)
+        finish_gate(last, 3, "ntc_bank")
+        finish_gate(last, 0, "ndc_bank")
+        quantise_gate(last, 3)
+        finish_gate(last, 1, "ndc_bank")
+        quantise_gate(last, 0)
+        finish_gate(last, 2, "ndc_bank")
+        quantise_gate(last, 1)
+        quantise_gate(last, 2)
+        for q in (3, 0, 1, 2):
+            add_passes(accs[q], ROUNDS - 1, q, (PASSES - 1,))
+        store(ROUNDS - 1, 3, accs[3], nc.scalar.copy, nc.scalar.dma_start)
+        store(ROUNDS - 1, 0, accs[0], nc.scalar.copy, nc.sync.dma_start)
+        store(ROUNDS - 1, 1, accs[1], nc.scalar.copy, nc.scalar.dma_start)
+        store(ROUNDS - 1, 2, accs[2], nc.vector.tensor_copy, nc.sync.dma_start)

@@ -32,9 +32,9 @@ FLOPS = 2 * TOKENS * (4 * H) * N_IN
 BYTES = TOKENS * 4 * H * 4 + 2 * TOKENS * H * 2 + BATCH * H * 2 + 4 * H * N_IN * 4
 
 LOAD_BUFS = {"i": 3, "g": 3, "f": 3, "o": 3, "grad": 5}
-X_QUANTISE_STEPS = (3, 5, 7, 9)
-FIRST_JOB_STEP = 9
-JOBS_A_STEP = 2
+X_PIECES = {1: (0,), 2: (1,), 3: (2,), 4: (3,), 5: (4, 5), 6: (6, 7)}
+X_QUANTISE_STEPS = (4, 5, 6, 7)
+MX_PASSES = {7: 3, 8: 6, 9: 6, 10: 6, 11: 6, 12: 6, 13: 6, 14: 6, 15: 3}
 
 
 def tile_lstmlayer_v_kernel(
@@ -165,8 +165,8 @@ def tile_lstmlayer_v_kernel(
         def turn_w(k):
             tiles[k]["w_bank"] = turned(tiles[k]["fiw"][:, part(2)], "w_bank", 1)
 
-        def turn_back_ntc(k):
-            tiles[k]["ntc_bank"] = turned(tiles[k]["ntc"], "ntc_bank", 2)
+        def turn_back_eo(k):
+            tiles[k]["eo_bank"] = turned(tiles[k]["eo"], "eo_bank", 1)
 
         def turn_back_ndc(k):
             tiles[k]["ndc_bank"] = turned(tiles[k]["ndc"], "ndc_bank", 1)
@@ -223,20 +223,29 @@ def tile_lstmlayer_v_kernel(
             )
 
         def factors(k):
-            tiles[k]["p"] = work.tile([P, 4 * CH], F32, name="factors", bufs=2)
+            tiles[k]["p"] = work.tile([P, 3 * CH], F32, name="factors", bufs=2)
 
         def factors_fi(k):
             t = tiles[k]
             minus_one_times(t["p"][:, 0 : 2 * CH], t["fiw"][:, 0 : 2 * CH], t["uv"][:])
 
-        def factors_go(k):
+        def factor_g(k):
             t = tiles[k]
-            minus_one_times(t["p"][:, 2 * CH : 4 * CH], t["go"][:], t["fiw"][:, CH : 3 * CH])
+            minus_one_times(t["p"][:, part(2)], t["go"][:, part(0)], t["fiw"][:, part(1)])
 
         def turned_dc(k):
             t = tiles[k]
             t["ndc"] = work.tile([P, CH], F32, name="ndc", bufs=2)
             minus_one_times(t["ndc"][:], t["tc2"][:], t["w_bank"][:])
+
+        def turned_eo(k):
+            t = tiles[k]
+            t["eo"] = work.tile([P, CH], F32, name="eo", bufs=2)
+            nc.vector.tensor_tensor(out=t["eo"][:], in0=t["ntc"][:], in1=t["w_bank"][:], op=ALU.mult)
+
+        def finish_o(k):
+            t = tiles[k]
+            minus_one_times(t["da"][:, part(3)], t["go"][:, part(1)], t["eo_bank"][:])
 
         def finish_gate(k, q, bank):
             t = tiles[k]
@@ -256,9 +265,7 @@ def tile_lstmlayer_v_kernel(
         def finish(k):
             t = tiles[k]
             new_da(k)
-            nc.vector.tensor_tensor(
-                out=t["da"][:, part(3)], in0=t["p"][:, part(3)], in1=t["ntc_bank"][:], op=ALU.mult
-            )
+            finish_o(k)
             nc.vector.tensor_tensor(
                 out=t["da"][:, 0 : 3 * CH].rearrange("p (n w) -> p n w", n=3),
                 in0=t["p"][:, 0 : 3 * CH].rearrange("p (n w) -> p n w", n=3),
@@ -278,11 +285,6 @@ def tile_lstmlayer_v_kernel(
                     start=(g == 0),
                     stop=(g == PASSES - 1),
                 )
-
-        def multiply(rnd, q):
-            acc = psum.tile([P, N_IN], F32, name="acc", bufs=2)
-            add_passes(acc, rnd, q, range(PASSES))
-            return acc
 
         def store(rnd, q, acc, copy, dma_start):
             result = work.tile([P, N_IN], F32, name="result", bufs=4)
@@ -315,23 +317,23 @@ def tile_lstmlayer_v_kernel(
         factors(0)
         factors_fi(0)
         gate_o(0)
+        product_v(1, nc.vector)
         make_w(0)
         turn_w(0)
         gate_f(1)
         tanh_c(0)
-        product_v(1, nc.vector)
         product_u(1, nc.vector)
         c_bank(1)
-        turn_back_ntc(0)
         square_g(0)
         gate_o(1)
         turned_dc(0)
+        turned_eo(0)
         turn_back_ndc(0)
-        factors_go(0)
+        turn_back_eo(0)
+        factor_g(0)
         make_w(1)
         turn_w(1)
         tanh_c(1)
-        turn_back_ntc(1)
         square_g(1)
         gate_ig(2)
         gate_f(2)
@@ -340,11 +342,14 @@ def tile_lstmlayer_v_kernel(
         gate_ig(3)
         finish(0)
         turned_dc(1)
+        turned_eo(1)
         turn_back_ndc(1)
-        product_v(2, nc.gpsimd)
-        product_u(2, nc.gpsimd)
+        turn_back_eo(1)
+        product_v(2, nc.vector)
+        product_u(2, nc.vector)
 
-        jobs = []
+        waiting = []
+        acc = None
         for k in range(1, CHUNKS):
             if k + 5 < CHUNKS:
                 load(k + 5, ("i", "g", "f", "o", "grad"))
@@ -354,7 +359,7 @@ def tile_lstmlayer_v_kernel(
                 load_x((k + 1) // 2)
             quantise(k - 1)
             if (k - 1) % PASSES == PASSES - 1:
-                jobs.extend([((k - 1) // PASSES, q) for q in range(4)])
+                waiting.extend([((k - 1) // PASSES, q, g) for q in range(4) for g in range(PASSES)])
             if (k + 3) % PASSES == 0 and k + 3 < CHUNKS:
                 regroup_c0((k + 3) // PASSES)
             if k + 2 < CHUNKS:
@@ -367,25 +372,30 @@ def tile_lstmlayer_v_kernel(
                 square_g(k + 2)
             if k + 3 < CHUNKS:
                 gate_ig(k + 3)
-            if k - 1 < 2 * PASSES:
-                x_piece(k - 1)
+            for m in X_PIECES.get(k, ()):
+                x_piece(m)
             factors(k)
-            factors_go(k)
-            if k in X_QUANTISE_STEPS:
-                x_quantise(X_QUANTISE_STEPS.index(k))
+            factor_g(k)
             factors_fi(k)
             if k + 1 < CHUNKS:
                 make_w(k + 1)
                 turn_w(k + 1)
-                turn_back_ntc(k + 1)
-            if k >= FIRST_JOB_STEP:
-                for job in jobs[:JOBS_A_STEP]:
-                    store(job[0], job[1], multiply(job[0], job[1]), nc.scalar.copy, nc.scalar.dma_start)
-                jobs = jobs[JOBS_A_STEP:]
+            passes = MX_PASSES.get(k, 0)
+            for rnd, q, g in waiting[:passes]:
+                if g == 0:
+                    acc = psum.tile([P, N_IN], F32, name="acc", bufs=3)
+                add_passes(acc, rnd, q, (g,))
+                if g == PASSES - 1:
+                    store(rnd, q, acc, nc.scalar.copy, nc.sync.dma_start)
+            waiting = waiting[passes:]
             if k + 1 < CHUNKS:
                 finish(k)
                 turned_dc(k + 1)
+                turned_eo(k + 1)
                 turn_back_ndc(k + 1)
+                turn_back_eo(k + 1)
+            if k in X_QUANTISE_STEPS:
+                x_quantise(X_QUANTISE_STEPS.index(k))
             if k + 2 < CHUNKS:
                 product_v(k + 2, nc.gpsimd)
                 product_u(k + 2, nc.gpsimd)
@@ -393,13 +403,13 @@ def tile_lstmlayer_v_kernel(
         last = CHUNKS - 1
         accs = {}
         for q in (3, 0):
-            accs[q] = psum.tile([P, N_IN], F32, name="acc", bufs=2)
+            accs[q] = psum.tile([P, N_IN], F32, name="acc", bufs=3)
         for q in (1, 2):
             accs[q] = psum.tile([P, N_IN], F32, name="c_bank", bufs=2)
         for q in (3, 0, 1, 2):
             add_passes(accs[q], ROUNDS - 1, q, range(PASSES - 1))
         new_da(last)
-        finish_gate(last, 3, "ntc_bank")
+        finish_o(last)
         finish_gate(last, 0, "ndc_bank")
         quantise_gate(last, 3)
         finish_gate(last, 1, "ndc_bank")

@@ -47,7 +47,7 @@ def tile_lstmlayer_v_kernel(
     dram["grad"] = grad_out.flatten_outer_dims()
 
     def by_partition(rows):
-        return rows.rearrange("(p j) w -> p j w", j=PACK)
+        return rows.rearrange("(j p) w -> p j w", j=PACK)
 
     def tokens_innermost(loaded):
         return loaded.rearrange("p j w -> p w j")
@@ -67,14 +67,13 @@ def tile_lstmlayer_v_kernel(
 
         x_codes = keep.tile([P, PASSES, N_IN], U32, align_bytes=64)
         x_scales = keep.tile([P, PASSES, N_IN], U8, align_bytes=64)
+        c0_tile = keep.tile([BATCH, H], BF16)
         identity = keep.tile([P, P], F32)
         make_identity(nc, identity[:])
 
         tiles = [{} for k in range(CHUNKS)]
         codes = {}
         scales = {}
-        c0_tiles = {}
-        c0_words = {}
         x_tiles = [{} for g in range(PASSES)]
 
         def load(k, names):
@@ -90,20 +89,6 @@ def tile_lstmlayer_v_kernel(
                     ),
                 )
                 tiles[k]["loaded_" + name] = loaded
-
-        def load_c0(rnd):
-            loaded = loads.tile([P, PACK, H_ROUND], BF16, name="loaded_c0", bufs=2)
-            for first_p in range(0, P, BATCH // PACK):
-                nc.sync.dma_start(
-                    out=loaded[first_p : first_p + BATCH // PACK],
-                    in_=by_partition(c0[:, rnd * H_ROUND : (rnd + 1) * H_ROUND]),
-                )
-            c0_tiles[rnd] = loaded
-
-        def regroup_c0(rnd):
-            words = work.tile([P, CH], BF16, name="c0_words", bufs=2)
-            nc.vector.tensor_copy(out=as_words(words[:]), in_=tokens_innermost(c0_tiles[rnd][:]))
-            c0_words[rnd] = words
 
         def load_x(g):
             loaded = loads.tile([P, PACK, N_IN], BF16, name="loaded_x", bufs=2)
@@ -142,8 +127,12 @@ def tile_lstmlayer_v_kernel(
 
         def product_u(k, engine):
             t = tiles[k]
+            columns = slice(k // PASSES * H_ROUND, (k // PASSES + 1) * H_ROUND)
             engine.tensor_tensor(
-                out=t["uv"][:, part(0)], in0=t["fiw"][:, part(0)], in1=c0_words[k // PASSES][:], op=ALU.mult
+                out=as_words(t["uv"][:, part(0)]),
+                in0=as_words(t["fiw"][:, part(0)]),
+                in1=c0_tile[:, columns].unsqueeze(2).to_broadcast([P, H_ROUND, PACK]),
+                op=ALU.mult,
             )
 
         def make_w(k):
@@ -298,18 +287,16 @@ def tile_lstmlayer_v_kernel(
         nc.scalar.activation(out=half_tile[:], in_=zero[:], func=ACT.Sigmoid)
 
         load(0, ("i", "g", "f"))
-        load_c0(0)
+        nc.sync.dma_start(out=c0_tile[:], in_=c0[:, :])
         load(1, ("i", "g"))
         load(0, ("o", "grad"))
         load(1, ("f", "o", "grad"))
         load(2, ("i", "g", "f", "o", "grad"))
-        load_c0(1)
         load_x(0)
         for k in range(3, 6):
             load(k, ("i", "g", "f", "o", "grad"))
         gate_ig(0)
         product_v(0, nc.vector)
-        regroup_c0(0)
         gate_f(0)
         product_u(0, nc.vector)
         c_bank(0)
@@ -353,15 +340,11 @@ def tile_lstmlayer_v_kernel(
         for k in range(1, CHUNKS):
             if k + 5 < CHUNKS:
                 load(k + 5, ("i", "g", "f", "o", "grad"))
-                if (k + 5) % PASSES == 2 and (k + 5) // PASSES + 1 < ROUNDS:
-                    load_c0((k + 5) // PASSES + 1)
             if (k + 1) % 2 == 0 and (k + 1) // 2 < PASSES:
                 load_x((k + 1) // 2)
             quantise(k - 1)
             if (k - 1) % PASSES == PASSES - 1:
                 waiting.extend([((k - 1) // PASSES, q, g) for q in range(4) for g in range(PASSES)])
-            if (k + 3) % PASSES == 0 and k + 3 < CHUNKS:
-                regroup_c0((k + 3) // PASSES)
             if k + 2 < CHUNKS:
                 gate_f(k + 2)
                 gate_o(k + 2)

@@ -31,10 +31,10 @@ BLOCKS = CH // P
 FLOPS = 2 * TOKENS * (4 * H) * N_IN
 BYTES = TOKENS * 4 * H * 4 + 2 * TOKENS * H * 2 + BATCH * H * 2 + 4 * H * N_IN * 4
 
-LOAD_BUFS = {"i": 3, "g": 3, "f": 3, "o": 3, "grad": 5}
+LOAD_BUFS = {"f": 4, "i": 4, "g": 4, "o": 4, "grad": 5}
 X_PIECES = {1: (0,), 2: (1,), 3: (2,), 4: (3,), 5: (4, 5), 6: (6, 7)}
 X_QUANTISE_STEPS = (4, 5, 6, 7)
-MX_PASSES = {7: 3, 8: 6, 9: 6, 10: 6, 11: 6, 12: 6, 13: 6, 14: 6, 15: 3}
+MX_PASSES = {7: 3, 8: 7, 9: 7, 10: 7, 11: 8, 12: 8, 13: 8}
 
 
 def tile_lstmlayer_v_kernel(
@@ -60,7 +60,7 @@ def tile_lstmlayer_v_kernel(
 
     with ExitStack() as stack:
         keep = stack.enter_context(tc.tile_pool(name="keep", bufs=1))
-        loads = stack.enter_context(tc.tile_pool(name="loads", bufs=3))
+        loads = stack.enter_context(tc.tile_pool(name="loads", bufs=4))
         work = stack.enter_context(tc.tile_pool(name="work", bufs=2))
         psum = stack.enter_context(tc.psum_pool(name="psum", bufs=1))
         stack.enter_context(tc.manual_schedule())
@@ -77,6 +77,8 @@ def tile_lstmlayer_v_kernel(
         x_tiles = [{} for g in range(PASSES)]
 
         def load(k, names):
+            if k >= CHUNKS:
+                return
             rnd, g = divmod(k, PASSES)
             for name in names:
                 loaded = loads.tile(
@@ -100,87 +102,137 @@ def tile_lstmlayer_v_kernel(
                 out=as_words(out_ap), in_=tokens_innermost(tiles[k]["loaded_" + gate][:]), func=func
             )
 
-        def start_chunk(k):
-            t = tiles[k]
-            t["fiw"] = work.tile([P, 3 * CH], F32, name="fiw", bufs=4)
-            t["go"] = work.tile([P, 2 * CH], F32, name="go", bufs=4)
-            t["g"] = work.tile([P, CH], F32, name="gate_g", bufs=3)
-
-        def gate_ig(k):
-            start_chunk(k)
-            activate(k, tiles[k]["fiw"][:, part(1)], "i", ACT.Sigmoid)
-            activate(k, tiles[k]["g"][:], "g", ACT.Tanh)
-
         def gate_f(k):
-            activate(k, tiles[k]["fiw"][:, part(0)], "f", ACT.Sigmoid)
+            tiles[k]["fi"] = work.tile([P, 2 * CH], F32, name="fi", bufs=4)
+            tiles[k]["ug"] = work.tile([P, 2 * CH], F32, name="ug", bufs=3)
+            activate(k, tiles[k]["fi"][:, part(0)], "f", ACT.Sigmoid)
+
+        def gate_i(k):
+            activate(k, tiles[k]["fi"][:, part(1)], "i", ACT.Sigmoid)
+
+        def gate_g(k):
+            activate(k, tiles[k]["ug"][:, part(1)], "g", ACT.Tanh)
 
         def gate_o(k):
+            tiles[k]["go"] = work.tile([P, 2 * CH], F32, name="go", bufs=5)
             activate(k, tiles[k]["go"][:, part(1)], "o", ACT.Sigmoid)
 
         def square_g(k):
-            nc.scalar.activation(out=tiles[k]["go"][:, part(0)], in_=tiles[k]["g"][:], func=ACT.Square)
-
-        def product_v(k, engine):
             t = tiles[k]
-            t["uv"] = work.tile([P, 2 * CH], F32, name="uv", bufs=2)
-            engine.tensor_tensor(out=t["uv"][:, part(1)], in0=t["fiw"][:, part(1)], in1=t["g"][:], op=ALU.mult)
+            nc.scalar.activation(out=t["go"][:, part(0)], in_=t["ug"][:, part(1)], func=ACT.Square)
+
+        def tanh_c(k):
+            t = tiles[k]
+            t["ntc"] = work.tile([P, CH], F32, name="ntc", bufs=3)
+            nc.scalar.activation(out=t["ntc"][:], in_=t["c"][:], func=ACT.Tanh, scale=-1.0)
+
+        def square_tanh(k):
+            t = tiles[k]
+            t["tc2"] = work.tile([P, CH], F32, name="tc_squared", bufs=3)
+            nc.scalar.activation(out=t["tc2"][:], in_=t["ntc"][:], func=ACT.Square)
 
         def product_u(k, engine):
             t = tiles[k]
             columns = slice(k // PASSES * H_ROUND, (k // PASSES + 1) * H_ROUND)
             engine.tensor_tensor(
-                out=as_words(t["uv"][:, part(0)]),
-                in0=as_words(t["fiw"][:, part(0)]),
+                out=as_words(t["ug"][:, part(0)]),
+                in0=as_words(t["fi"][:, part(0)]),
                 in1=c0_tile[:, columns].unsqueeze(2).to_broadcast([P, H_ROUND, PACK]),
                 op=ALU.mult,
             )
 
-        def make_w(k):
+        def product_w(k, engine):
             t = tiles[k]
-            nc.vector.tensor_tensor(
-                out=as_words(t["fiw"][:, part(2)]),
+            engine.tensor_tensor(
+                out=as_words(t["fi"][:, part(0)]),
                 in0=as_words(t["go"][:, part(1)]),
                 in1=tokens_innermost(t["loaded_grad"][:]),
                 op=ALU.mult,
             )
 
-        def turned(source, name, bufs):
-            bank = psum.tile([P, CH], F32, name=name, bufs=bufs)
+        def minus_one_times(out_ap, in0, in1):
+            nc.vector.scalar_tensor_tensor(
+                out=out_ap, in0=in0, scalar=1.0, in1=in1, op0=ALU.subtract, op1=ALU.mult
+            )
+
+        def times(out_ap, in0, in1):
+            nc.vector.tensor_tensor(out=out_ap, in0=in0, in1=in1, op=ALU.mult)
+
+        def factors(k):
+            t = tiles[k]
+            t["p"] = work.tile([P, 2 * CH], F32, name="factors", bufs=3)
+            minus_one_times(t["p"][:], t["fi"][:], t["ug"][:])
+
+        def turned(source, name):
+            bank = psum.tile([P, CH], F32, name=name, bufs=1)
             for b in range(BLOCKS):
                 cols = slice(b * P, (b + 1) * P)
                 nc.tensor.transpose(out=bank[:, cols], in_=source[:, cols], identity=identity[:])
             return bank
 
         def turn_w(k):
-            tiles[k]["w_bank"] = turned(tiles[k]["fiw"][:, part(2)], "w_bank", 1)
+            tiles[k]["w_bank"] = turned(tiles[k]["fi"][:, part(0)], "w_bank")
 
-        def turn_back_eo(k):
-            tiles[k]["eo_bank"] = turned(tiles[k]["eo"], "eo_bank", 1)
+        def turn_i(k):
+            tiles[k]["i_bank"] = turned(tiles[k]["fi"][:, part(1)], "i_bank")
 
-        def turn_back_ndc(k):
-            tiles[k]["ndc_bank"] = turned(tiles[k]["ndc"], "ndc_bank", 1)
+        def turn_back(k):
+            for name in ("eo", "ndc", "eg"):
+                tiles[k][name + "_bank"] = turned(tiles[k][name], name + "_bank")
 
         def c_bank(k):
             t = tiles[k]
-            t["c"] = psum.tile([P, CH], F32, name="c_bank", bufs=2)
+            t["c"] = psum.tile([P, CH], F32, name="c_bank", bufs=1)
             for b in range(BLOCKS):
-                cols = slice(b * P, (b + 1) * P)
-                for n in range(2):
+                terms = (
+                    t["ug"][:, b * P : (b + 1) * P],
+                    t["ug"][:, CH + b * P : CH + (b + 1) * P],
+                    t["p"][:, CH + b * P : CH + (b + 1) * P],
+                )
+                for n, term in enumerate(terms):
                     nc.tensor.matmul(
-                        out=t["c"][:, cols],
-                        lhsT=t["uv"][:, n * CH + b * P : n * CH + (b + 1) * P],
+                        out=t["c"][:, b * P : (b + 1) * P],
+                        lhsT=term,
                         rhs=identity[:],
                         is_transpose=True,
                         start=(n == 0),
-                        stop=(n == 1),
+                        stop=(n == len(terms) - 1),
                     )
 
-        def tanh_c(k):
+        def turned_products(k):
             t = tiles[k]
-            t["ntc"] = work.tile([P, CH], F32, name="ntc", bufs=2)
-            nc.scalar.activation(out=t["ntc"][:], in_=t["c"][:], func=ACT.Tanh, scale=-1.0)
-            t["tc2"] = work.tile([P, CH], F32, name="tc_squared", bufs=2)
-            nc.scalar.activation(out=t["tc2"][:], in_=t["ntc"][:], func=ACT.Square)
+            for name in ("ndc", "eo", "eg"):
+                t[name] = work.tile([P, CH], F32, name=name, bufs=2)
+            minus_one_times(t["ndc"][:], t["tc2"][:], t["w_bank"][:])
+            times(t["eo"][:], t["ntc"][:], t["w_bank"][:])
+            times(t["eg"][:], t["ndc"][:], t["i_bank"][:])
+
+        def new_da(k):
+            tiles[k]["da"] = work.tile([P, 4 * CH], BF16, name="da", bufs=2, align_bytes=64)
+
+        def finish_gate(k, q):
+            t = tiles[k]
+            da = t["da"][:, part(q)]
+            if q == 0:
+                times(da, t["p"][:, part(0)], t["ndc_bank"][:])
+            elif q == 1:
+                times(da, t["p"][:, part(1)], t["eg_bank"][:])
+            elif q == 2:
+                minus_one_times(da, t["go"][:, part(0)], t["eg_bank"][:])
+            else:
+                minus_one_times(da, t["go"][:, part(1)], t["eo_bank"][:])
+
+        def quantise_part(k, first, last):
+            rnd, g = divmod(k, PASSES)
+            if rnd not in codes:
+                codes[rnd] = work.tile([P, PASSES, CH], U32, name="codes", bufs=3, align_bytes=64)
+                scales[rnd] = work.tile([P, PASSES, CH], U8, name="scales", bufs=3, align_bytes=64)
+            columns = slice(first * H_ROUND, last * H_ROUND)
+            nc.vector.quantize_mx(
+                out=codes[rnd][:, g, columns].bitcast(E5M2_X4),
+                scales=scales[rnd][:, g, columns],
+                in_=tiles[k]["da"][:, first * CH : last * CH],
+            )
 
         def x_piece(m):
             g, half = divmod(m, 2)
@@ -195,71 +247,6 @@ def tile_lstmlayer_v_kernel(
         def x_quantise(g):
             nc.vector.quantize_mx(
                 out=x_codes[:, g, :].bitcast(E4M3_X4), scales=x_scales[:, g, :], in_=x_tiles[g]["words"][:]
-            )
-
-        def quantise(k):
-            rnd, g = divmod(k, PASSES)
-            if g == 0:
-                codes[rnd] = work.tile([P, PASSES, CH], U32, name="codes", bufs=3, align_bytes=64)
-                scales[rnd] = work.tile([P, PASSES, CH], U8, name="scales", bufs=3, align_bytes=64)
-            nc.vector.quantize_mx(
-                out=codes[rnd][:, g, :].bitcast(E5M2_X4), scales=scales[rnd][:, g, :], in_=tiles[k]["da"][:]
-            )
-
-        def minus_one_times(out_ap, in0, in1):
-            nc.vector.scalar_tensor_tensor(
-                out=out_ap, in0=in0, scalar=1.0, in1=in1, op0=ALU.subtract, op1=ALU.mult
-            )
-
-        def factors(k):
-            tiles[k]["p"] = work.tile([P, 3 * CH], F32, name="factors", bufs=2)
-
-        def factors_fi(k):
-            t = tiles[k]
-            minus_one_times(t["p"][:, 0 : 2 * CH], t["fiw"][:, 0 : 2 * CH], t["uv"][:])
-
-        def factor_g(k):
-            t = tiles[k]
-            minus_one_times(t["p"][:, part(2)], t["go"][:, part(0)], t["fiw"][:, part(1)])
-
-        def turned_dc(k):
-            t = tiles[k]
-            t["ndc"] = work.tile([P, CH], F32, name="ndc", bufs=2)
-            minus_one_times(t["ndc"][:], t["tc2"][:], t["w_bank"][:])
-
-        def turned_eo(k):
-            t = tiles[k]
-            t["eo"] = work.tile([P, CH], F32, name="eo", bufs=2)
-            nc.vector.tensor_tensor(out=t["eo"][:], in0=t["ntc"][:], in1=t["w_bank"][:], op=ALU.mult)
-
-        def finish_o(k):
-            t = tiles[k]
-            minus_one_times(t["da"][:, part(3)], t["go"][:, part(1)], t["eo_bank"][:])
-
-        def finish_gate(k, q, bank):
-            t = tiles[k]
-            nc.vector.tensor_tensor(out=t["da"][:, part(q)], in0=t["p"][:, part(q)], in1=t[bank][:], op=ALU.mult)
-
-        def quantise_gate(k, q):
-            rnd, g = divmod(k, PASSES)
-            nc.vector.quantize_mx(
-                out=codes[rnd][:, g, q * H_ROUND : (q + 1) * H_ROUND].bitcast(E5M2_X4),
-                scales=scales[rnd][:, g, q * H_ROUND : (q + 1) * H_ROUND],
-                in_=tiles[k]["da"][:, part(q)],
-            )
-
-        def new_da(k):
-            tiles[k]["da"] = work.tile([P, 4 * CH], BF16, name="da", bufs=2, align_bytes=64)
-
-        def finish(k):
-            t = tiles[k]
-            new_da(k)
-            finish_o(k)
-            nc.vector.tensor_tensor(
-                out=t["da"][:, 0 : 3 * CH].rearrange("p (n w) -> p n w", n=3),
-                in0=t["p"][:, 0 : 3 * CH].rearrange("p (n w) -> p n w", n=3),
-                in1=t["ndc_bank"][:].unsqueeze(1).to_broadcast([P, 3, CH]),
-                op=ALU.mult,
             )
 
         def add_passes(acc, rnd, q, passes):
@@ -286,123 +273,122 @@ def tile_lstmlayer_v_kernel(
         nc.vector.memset(zero[:], 0.0)
         nc.scalar.activation(out=half_tile[:], in_=zero[:], func=ACT.Sigmoid)
 
-        load(0, ("i", "g", "f"))
+        load(0, ("f",))
         nc.sync.dma_start(out=c0_tile[:], in_=c0[:, :])
-        load(1, ("i", "g"))
+        load(0, ("i", "g"))
+        load(1, ("f", "i", "g"))
         load(0, ("o", "grad"))
-        load(1, ("f", "o", "grad"))
-        load(2, ("i", "g", "f", "o", "grad"))
+        load(1, ("o", "grad"))
+        load(2, ("f", "i", "g", "o", "grad"))
+        load(3, ("f", "i", "g", "o", "grad"))
         load_x(0)
-        for k in range(3, 6):
-            load(k, ("i", "g", "f", "o", "grad"))
-        gate_ig(0)
-        product_v(0, nc.vector)
+        load(4, ("f", "i", "g", "o", "grad"))
+        load(5, ("f", "i", "g", "o", "grad"))
+
         gate_f(0)
+        gate_i(0)
+        gate_g(0)
         product_u(0, nc.vector)
-        c_bank(0)
-        gate_ig(1)
         factors(0)
-        factors_fi(0)
-        gate_o(0)
-        product_v(1, nc.vector)
-        make_w(0)
-        turn_w(0)
+        c_bank(0)
+        turn_i(0)
         gate_f(1)
-        tanh_c(0)
+        gate_i(1)
+        gate_g(1)
         product_u(1, nc.vector)
+        factors(1)
+        gate_o(0)
+        product_w(0, nc.vector)
+        turn_w(0)
         c_bank(1)
-        square_g(0)
+        tanh_c(0)
         gate_o(1)
-        turned_dc(0)
-        turned_eo(0)
-        turn_back_ndc(0)
-        turn_back_eo(0)
-        factor_g(0)
-        make_w(1)
-        turn_w(1)
-        tanh_c(1)
-        square_g(1)
-        gate_ig(2)
+        square_tanh(0)
         gate_f(2)
+        gate_i(2)
+        gate_g(2)
+        tanh_c(1)
+        square_g(0)
+        square_tanh(1)
         gate_o(2)
+        square_g(1)
         square_g(2)
-        gate_ig(3)
-        finish(0)
-        turned_dc(1)
-        turned_eo(1)
-        turn_back_ndc(1)
-        turn_back_eo(1)
-        product_v(2, nc.vector)
+        turned_products(0)
+        turn_back(0)
+        product_w(1, nc.vector)
         product_u(2, nc.vector)
 
         waiting = []
         acc = None
-        for k in range(1, CHUNKS):
-            if k + 5 < CHUNKS:
-                load(k + 5, ("i", "g", "f", "o", "grad"))
-            if (k + 1) % 2 == 0 and (k + 1) // 2 < PASSES:
+        accs = {}
+        for k in range(CHUNKS - 1):
+            load(k + 6, ("f", "i", "g", "o", "grad"))
+            if k % 2 == 1 and (k + 1) // 2 < PASSES:
                 load_x((k + 1) // 2)
-            quantise(k - 1)
-            if (k - 1) % PASSES == PASSES - 1:
-                waiting.extend([((k - 1) // PASSES, q, g) for q in range(4) for g in range(PASSES)])
-            if k + 2 < CHUNKS:
-                gate_f(k + 2)
-                gate_o(k + 2)
-            if k + 1 < CHUNKS:
-                c_bank(k + 1)
-                tanh_c(k + 1)
-            if k + 2 < CHUNKS:
-                square_g(k + 2)
+            if k >= 1:
+                quantise_part(k - 1, 0, 4)
+                if k % PASSES == 0:
+                    waiting.extend([(k // PASSES - 1, q, g) for q in range(4) for g in range(PASSES)])
             if k + 3 < CHUNKS:
-                gate_ig(k + 3)
-            for m in X_PIECES.get(k, ()):
-                x_piece(m)
-            factors(k)
-            factor_g(k)
-            factors_fi(k)
-            if k + 1 < CHUNKS:
-                make_w(k + 1)
-                turn_w(k + 1)
+                gate_f(k + 3)
+                gate_i(k + 3)
+                gate_g(k + 3)
+            turn_w(k + 1)
+            turn_i(k + 1)
             passes = MX_PASSES.get(k, 0)
             for rnd, q, g in waiting[:passes]:
                 if g == 0:
-                    acc = psum.tile([P, N_IN], F32, name="acc", bufs=3)
+                    acc = psum.tile([P, N_IN], F32, name="acc", bufs=2)
                 add_passes(acc, rnd, q, (g,))
                 if g == PASSES - 1:
                     store(rnd, q, acc, nc.scalar.copy, nc.sync.dma_start)
             waiting = waiting[passes:]
-            if k + 1 < CHUNKS:
-                finish(k)
-                turned_dc(k + 1)
-                turned_eo(k + 1)
-                turn_back_ndc(k + 1)
-                turn_back_eo(k + 1)
+            if k == CHUNKS - 2:
+                for q, tag, bufs in ((3, "acc", 2), (0, "acc", 2), (1, "c_bank", 1)):
+                    accs[q] = psum.tile([P, N_IN], F32, name=tag, bufs=bufs)
+                    add_passes(accs[q], ROUNDS - 1, q, range(PASSES - 2))
+            if k + 3 < CHUNKS:
+                gate_o(k + 3)
+                square_g(k + 3)
+            if k + 2 < CHUNKS:
+                factors(k + 2)
+                c_bank(k + 2)
+                tanh_c(k + 2)
+            for m in X_PIECES.get(k, ()):
+                x_piece(m)
+            if k + 2 < CHUNKS:
+                square_tanh(k + 2)
+            new_da(k)
+            for q in (3, 0, 1, 2):
+                finish_gate(k, q)
+            turned_products(k + 1)
+            turn_back(k + 1)
             if k in X_QUANTISE_STEPS:
                 x_quantise(X_QUANTISE_STEPS.index(k))
             if k + 2 < CHUNKS:
-                product_v(k + 2, nc.gpsimd)
-                product_u(k + 2, nc.gpsimd)
+                product_w(k + 2, nc.gpsimd)
+            if k + 3 < CHUNKS:
+                product_u(k + 3, nc.gpsimd)
 
         last = CHUNKS - 1
-        accs = {}
-        for q in (3, 0):
-            accs[q] = psum.tile([P, N_IN], F32, name="acc", bufs=3)
-        for q in (1, 2):
-            accs[q] = psum.tile([P, N_IN], F32, name="c_bank", bufs=2)
-        for q in (3, 0, 1, 2):
-            add_passes(accs[q], ROUNDS - 1, q, range(PASSES - 1))
+        rnd = ROUNDS - 1
+        quantise_part(last - 1, 0, 4)
+        for q in (3, 0, 1):
+            add_passes(accs[q], rnd, q, (PASSES - 2,))
+        accs[2] = psum.tile([P, N_IN], F32, name="w_bank", bufs=1)
+        add_passes(accs[2], rnd, 2, range(PASSES - 1))
         new_da(last)
-        finish_o(last)
-        finish_gate(last, 0, "ndc_bank")
-        quantise_gate(last, 3)
-        finish_gate(last, 1, "ndc_bank")
-        quantise_gate(last, 0)
-        finish_gate(last, 2, "ndc_bank")
-        quantise_gate(last, 1)
-        quantise_gate(last, 2)
+        finish_gate(last, 3)
+        finish_gate(last, 0)
+        quantise_part(last, 3, 4)
+        finish_gate(last, 1)
+        quantise_part(last, 0, 1)
+        finish_gate(last, 2)
+        quantise_part(last, 1, 2)
+        quantise_part(last, 2, 3)
         for q in (3, 0, 1, 2):
-            add_passes(accs[q], ROUNDS - 1, q, (PASSES - 1,))
-        store(ROUNDS - 1, 3, accs[3], nc.scalar.copy, nc.scalar.dma_start)
-        store(ROUNDS - 1, 0, accs[0], nc.scalar.copy, nc.sync.dma_start)
-        store(ROUNDS - 1, 1, accs[1], nc.scalar.copy, nc.scalar.dma_start)
-        store(ROUNDS - 1, 2, accs[2], nc.vector.tensor_copy, nc.sync.dma_start)
+            add_passes(accs[q], rnd, q, (PASSES - 1,))
+        store(rnd, 3, accs[3], nc.scalar.copy, nc.scalar.dma_start)
+        store(rnd, 0, accs[0], nc.scalar.copy, nc.sync.dma_start)
+        store(rnd, 1, accs[1], nc.scalar.copy, nc.scalar.dma_start)
+        store(rnd, 2, accs[2], nc.vector.tensor_copy, nc.sync.dma_start)

@@ -55,6 +55,12 @@ def tile_lstmlayer_v_kernel(
     def as_words(flat):
         return flat.rearrange("p (w j) -> p w j", j=PACK)
 
+    def loaded_by_four(loaded):
+        return loaded.rearrange("p j (c i) -> p c j i", i=4)
+
+    def words_by_four(flat):
+        return flat.rearrange("p (c i j) -> p c j i", i=4, j=PACK)
+
     def part(n):
         return slice(n * CH, (n + 1) * CH)
 
@@ -93,13 +99,13 @@ def tile_lstmlayer_v_kernel(
                 tiles[k]["loaded_" + name] = loaded
 
         def load_x(g):
-            loaded = loads.tile([P, PACK, N_IN], BF16, name="loaded_x", bufs=2)
+            loaded = loads.tile([P, PACK, N_IN], BF16, name="loaded_x", bufs=3)
             nc.sync.dma_start(out=loaded[:], in_=by_partition(x_rows[g * K_PASS : (g + 1) * K_PASS, :]))
             x_tiles[g]["loaded"] = loaded
 
         def activate(k, out_ap, gate, func):
             nc.scalar.activation(
-                out=as_words(out_ap), in_=tokens_innermost(tiles[k]["loaded_" + gate][:]), func=func
+                out=words_by_four(out_ap), in_=loaded_by_four(tiles[k]["loaded_" + gate][:]), func=func
             )
 
         def gate_f(k):
@@ -240,8 +246,8 @@ def tile_lstmlayer_v_kernel(
             if half == 0:
                 x_tiles[g]["words"] = work.tile([P, N_IN * PACK], BF16, name="x_words", bufs=2, align_bytes=64)
             nc.scalar.copy(
-                out=as_words(x_tiles[g]["words"][:, half * cols * PACK : (half + 1) * cols * PACK]),
-                in_=tokens_innermost(x_tiles[g]["loaded"][:, :, half * cols : (half + 1) * cols]),
+                out=words_by_four(x_tiles[g]["words"][:, half * cols * PACK : (half + 1) * cols * PACK]),
+                in_=loaded_by_four(x_tiles[g]["loaded"][:, :, half * cols : (half + 1) * cols]),
             )
 
         def x_quantise(g):
@@ -315,7 +321,7 @@ def tile_lstmlayer_v_kernel(
         square_g(2)
         turned_products(0)
         turn_back(0)
-        product_w(1, nc.vector)
+        product_w(1, nc.gpsimd)
         product_u(2, nc.vector)
 
         waiting = []
@@ -323,8 +329,8 @@ def tile_lstmlayer_v_kernel(
         accs = {}
         for k in range(CHUNKS - 1):
             load(k + 6, ("f", "i", "g", "o", "grad"))
-            if k % 2 == 1 and (k + 1) // 2 < PASSES:
-                load_x((k + 1) // 2)
+            if k % 2 == 0 and k // 2 + 1 < PASSES:
+                load_x(k // 2 + 1)
             if k >= 1:
                 quantise_part(k - 1, 0, 4)
                 if k % PASSES == 0:

@@ -34,6 +34,8 @@ BYTES = TOKENS * 4 * H * 4 + 2 * TOKENS * H * 2 + BATCH * H * 2 + 4 * H * N_IN *
 LOAD_BUFS = {"f": 4, "i": 4, "g": 4, "o": 4, "grad": 5}
 X_PIECES = {1: (0,), 2: (1,), 3: (2,), 4: (3,), 5: (4, 5), 6: (6, 7)}
 X_QUANTISE_STEPS = (4, 5, 6, 7)
+G_COLS = CH // 4
+FIRST_G = 3
 MX_PASSES = {7: 3, 8: 7, 9: 7, 10: 7, 11: 8, 12: 8, 13: 8}
 
 
@@ -110,8 +112,15 @@ def tile_lstmlayer_v_kernel(
 
         def gate_f(k):
             tiles[k]["fi"] = work.tile([P, 2 * CH], F32, name="fi", bufs=4)
-            tiles[k]["ug"] = work.tile([P, 2 * CH], F32, name="ug", bufs=3)
+            tiles[k]["ug"] = work.tile([P, 2 * CH], F32, name="ug", bufs=4)
             activate(k, tiles[k]["fi"][:, part(0)], "f", ACT.Sigmoid)
+
+        def f_minus_one(k):
+            t = tiles[k]
+            t["fm1"] = work.tile([P, G_COLS], F32, name="fm1", bufs=4)
+            nc.scalar.activation(
+                out=t["fm1"][:], in_=t["fi"][:, 0:G_COLS], func=ACT.Identity, bias=-1.0
+            )
 
         def gate_i(k):
             activate(k, tiles[k]["fi"][:, part(1)], "i", ACT.Sigmoid)
@@ -167,7 +176,14 @@ def tile_lstmlayer_v_kernel(
         def factors(k):
             t = tiles[k]
             t["p"] = work.tile([P, 2 * CH], F32, name="factors", bufs=3)
-            minus_one_times(t["p"][:], t["fi"][:], t["ug"][:])
+            first = G_COLS if k >= FIRST_G else 0
+            minus_one_times(t["p"][:, first:], t["fi"][:, first:], t["ug"][:, first:])
+
+        def factors_on_gpsimd(k):
+            t = tiles[k]
+            nc.gpsimd.tensor_tensor(
+                out=t["p"][:, 0:G_COLS], in0=t["fm1"][:], in1=t["ug"][:, 0:G_COLS], op=ALU.mult
+            )
 
         def turned(source, name):
             bank = psum.tile([P, CH], F32, name=name, bufs=1)
@@ -205,13 +221,15 @@ def tile_lstmlayer_v_kernel(
                         stop=(n == len(terms) - 1),
                     )
 
-        def turned_products(k):
+        def turned_product(k, name):
             t = tiles[k]
-            for name in ("ndc", "eo", "eg"):
-                t[name] = work.tile([P, CH], F32, name=name, bufs=2)
-            minus_one_times(t["ndc"][:], t["tc2"][:], t["w_bank"][:])
-            times(t["eo"][:], t["ntc"][:], t["w_bank"][:])
-            times(t["eg"][:], t["ndc"][:], t["i_bank"][:])
+            t[name] = work.tile([P, CH], F32, name=name, bufs=2)
+            if name == "ndc":
+                minus_one_times(t["ndc"][:], t["tc2"][:], t["w_bank"][:])
+            elif name == "eo":
+                times(t["eo"][:], t["ntc"][:], t["w_bank"][:])
+            else:
+                times(t["eg"][:], t["ndc"][:], t["i_bank"][:])
 
         def new_da(k):
             tiles[k]["da"] = work.tile([P, 4 * CH], BF16, name="da", bufs=2, align_bytes=64)
@@ -308,21 +326,21 @@ def tile_lstmlayer_v_kernel(
         turn_w(0)
         c_bank(1)
         tanh_c(0)
-        gate_o(1)
         square_tanh(0)
+        gate_o(1)
         gate_f(2)
         gate_i(2)
         gate_g(2)
         tanh_c(1)
+        gate_o(2)
         square_g(0)
         square_tanh(1)
-        gate_o(2)
-        square_g(1)
-        square_g(2)
-        turned_products(0)
-        turn_back(0)
+        turned_product(0, "eo")
+        turned_product(0, "ndc")
         product_w(1, nc.gpsimd)
         product_u(2, nc.vector)
+        turned_product(0, "eg")
+        turn_back(0)
 
         waiting = []
         acc = None
@@ -339,6 +357,7 @@ def tile_lstmlayer_v_kernel(
                 gate_f(k + 3)
                 gate_i(k + 3)
                 gate_g(k + 3)
+                f_minus_one(k + 3)
             turn_w(k + 1)
             turn_i(k + 1)
             passes = MX_PASSES.get(k, 0)
@@ -355,7 +374,7 @@ def tile_lstmlayer_v_kernel(
                     add_passes(accs[q], ROUNDS - 1, q, range(PASSES - 2))
             if k + 3 < CHUNKS:
                 gate_o(k + 3)
-                square_g(k + 3)
+            square_g(k + 1)
             if k + 2 < CHUNKS:
                 factors(k + 2)
                 c_bank(k + 2)
@@ -367,7 +386,8 @@ def tile_lstmlayer_v_kernel(
             new_da(k)
             for q in (3, 0, 1, 2):
                 finish_gate(k, q)
-            turned_products(k + 1)
+            for name in ("ndc", "eo", "eg"):
+                turned_product(k + 1, name)
             turn_back(k + 1)
             if k in X_QUANTISE_STEPS:
                 x_quantise(X_QUANTISE_STEPS.index(k))
@@ -375,6 +395,8 @@ def tile_lstmlayer_v_kernel(
                 product_w(k + 2, nc.gpsimd)
             if k + 3 < CHUNKS:
                 product_u(k + 3, nc.gpsimd)
+            if FIRST_G <= k + 2 < CHUNKS:
+                factors_on_gpsimd(k + 2)
 
         last = CHUNKS - 1
         rnd = ROUNDS - 1

@@ -177,7 +177,8 @@ def tile_lstmlayer_v_kernel(
             t = tiles[k]
             t["p"] = work.tile([P, 2 * CH], F32, name="factors", bufs=3)
             first = G_COLS if k >= FIRST_G else 0
-            minus_one_times(t["p"][:, first:], t["fi"][:, first:], t["ug"][:, first:])
+            for columns in (slice(first, CH), part(1)):
+                minus_one_times(t["p"][:, columns], t["fi"][:, columns], t["ug"][:, columns])
 
         def factors_on_gpsimd(k):
             t = tiles[k]

@@ -35,6 +35,7 @@ LOAD_BUFS = {"f": 4, "i": 4, "g": 4, "o": 4, "grad": 5}
 X_PIECES = {1: (0,), 2: (1,), 3: (2,), 4: (3,), 5: (4, 5), 6: (6, 7)}
 X_QUANTISE_STEPS = (4, 5, 6, 7)
 G_COLS = CH // 4
+GPSIMD_FINISH = (13, 14)
 FIRST_G = 3
 MX_PASSES = {7: 3, 8: 7, 9: 7, 10: 7, 11: 8, 12: 8, 13: 8}
 
@@ -176,7 +177,7 @@ def tile_lstmlayer_v_kernel(
         def factors(k):
             t = tiles[k]
             t["p"] = work.tile([P, 2 * CH], F32, name="factors", bufs=3)
-            first = G_COLS if k >= FIRST_G else 0
+            first = G_COLS if FIRST_G <= k < CHUNKS - 1 else 0
             for columns in (slice(first, CH), part(1)):
                 minus_one_times(t["p"][:, columns], t["fi"][:, columns], t["ug"][:, columns])
 
@@ -247,6 +248,17 @@ def tile_lstmlayer_v_kernel(
             else:
                 minus_one_times(da, t["go"][:, part(1)], t["eo_bank"][:])
 
+        def copy_ndc(k):
+            t = tiles[k]
+            t["ndc_copy"] = work.tile([P, CH], F32, name="ndc_copy", bufs=2)
+            nc.scalar.copy(out=t["ndc_copy"][:], in_=t["ndc_bank"][:])
+
+        def finish_f_on_gpsimd(k):
+            t = tiles[k]
+            nc.gpsimd.tensor_tensor(
+                out=t["da"][:, part(0)], in0=t["p"][:, part(0)], in1=t["ndc_copy"][:], op=ALU.mult
+            )
+
         def quantise_part(k, first, last):
             rnd, g = divmod(k, PASSES)
             if rnd not in codes:
@@ -301,9 +313,9 @@ def tile_lstmlayer_v_kernel(
         load(0, ("f",))
         nc.sync.dma_start(out=c0_tile[:], in_=c0[:, :])
         load(0, ("i", "g"))
-        load(1, ("f", "i", "g"))
+        load(1, ("f",))
         load(0, ("o", "grad"))
-        load(1, ("o", "grad"))
+        load(1, ("i", "g", "o", "grad"))
         load(2, ("f", "i", "g", "o", "grad"))
         load(3, ("f", "i", "g", "o", "grad"))
         load_x(0)
@@ -318,13 +330,13 @@ def tile_lstmlayer_v_kernel(
         c_bank(0)
         turn_i(0)
         gate_f(1)
-        gate_i(1)
-        gate_g(1)
         product_u(1, nc.vector)
-        factors(1)
         gate_o(0)
         product_w(0, nc.vector)
         turn_w(0)
+        gate_i(1)
+        gate_g(1)
+        factors(1)
         c_bank(1)
         tanh_c(0)
         square_tanh(0)
@@ -338,7 +350,7 @@ def tile_lstmlayer_v_kernel(
         square_tanh(1)
         turned_product(0, "eo")
         turned_product(0, "ndc")
-        product_w(1, nc.gpsimd)
+        product_w(1, nc.vector)
         product_u(2, nc.vector)
         turned_product(0, "eg")
         turn_back(0)
@@ -354,6 +366,8 @@ def tile_lstmlayer_v_kernel(
                 quantise_part(k - 1, 0, 4)
                 if k % PASSES == 0:
                     waiting.extend([(k // PASSES - 1, q, g) for q in range(4) for g in range(PASSES)])
+            if k in GPSIMD_FINISH:
+                copy_ndc(k)
             if k + 3 < CHUNKS:
                 gate_f(k + 3)
                 gate_i(k + 3)
@@ -385,7 +399,7 @@ def tile_lstmlayer_v_kernel(
             if k + 2 < CHUNKS:
                 square_tanh(k + 2)
             new_da(k)
-            for q in (3, 0, 1, 2):
+            for q in (3, 1, 2) if k in GPSIMD_FINISH else (3, 0, 1, 2):
                 finish_gate(k, q)
             for name in ("ndc", "eo", "eg"):
                 turned_product(k + 1, name)
@@ -394,9 +408,11 @@ def tile_lstmlayer_v_kernel(
                 x_quantise(X_QUANTISE_STEPS.index(k))
             if k + 2 < CHUNKS:
                 product_w(k + 2, nc.gpsimd)
+            if k in GPSIMD_FINISH:
+                finish_f_on_gpsimd(k)
             if k + 3 < CHUNKS:
                 product_u(k + 3, nc.gpsimd)
-            if FIRST_G <= k + 2 < CHUNKS:
+            if FIRST_G <= k + 2 < CHUNKS - 1:
                 factors_on_gpsimd(k + 2)
 
         last = CHUNKS - 1

from contextlib import ExitStack

import concourse.mybir as mybir
from concourse.masks import make_identity

F32 = mybir.dt.float32
BF16 = mybir.dt.bfloat16
U32 = mybir.dt.uint32
U8 = mybir.dt.uint8
E4M3_X4 = mybir.dt.float8_e4m3fn_x4
E5M2_X4 = mybir.dt.float8_e5m2_x4
ACT = mybir.ActivationFunctionType
ALU = mybir.AluOpType

P = 128
PACK = 4
K_PASS = P * PACK
BATCH = 128
TOKENS = 16 * BATCH
PASSES = TOKENS // K_PASS
H = 512
N_IN = 512
GATES = ("i", "f", "g", "o")
DA_ORDER = ("f", "i", "g", "o")
H_ROUND = P
ROUNDS = H // H_ROUND
CHUNKS = ROUNDS * PASSES
CH = H_ROUND * PACK
BLOCKS = CH // P

FLOPS = 2 * TOKENS * (4 * H) * N_IN
BYTES = TOKENS * 4 * H * 4 + 2 * TOKENS * H * 2 + BATCH * H * 2 + 4 * H * N_IN * 4

LOAD_BUFS = {"f": 4, "i": 4, "g": 4, "o": 4, "grad": 5}
X_PIECES = {1: (0,), 2: (1,), 3: (2,), 4: (3,), 5: (4, 5), 6: (6, 7)}
X_QUANTISE_STEPS = (4, 5, 6, 7)
G_COLS = CH // 4
GPSIMD_FINISH = (13, 14)
FIRST_G = 3
MX_PASSES = {7: 3, 8: 7, 9: 7, 10: 7, 11: 8, 12: 8, 13: 8}


def tile_lstmlayer_v_kernel(
    tc, x, h0, c0, noise, w_ih, w_hh, b_ih, b_hh, gates, grad_out, out
):
    nc = tc.nc
    x_rows = x.flatten_outer_dims()
    gates_rows = gates.flatten_outer_dims()
    dram = {gate: gates_rows[:, q * H : (q + 1) * H] for q, gate in enumerate(GATES)}
    dram["grad"] = grad_out.flatten_outer_dims()

    def by_partition(rows):
        return rows.rearrange("(j p) w -> p j w", j=PACK)

    def tokens_innermost(loaded):
        return loaded.rearrange("p j w -> p w j")

    def as_words(flat):
        return flat.rearrange("p (w j) -> p w j", j=PACK)

    def loaded_by_four(loaded):
        return loaded.rearrange("p j (c i) -> p c j i", i=4)

    def words_by_four(flat):
        return flat.rearrange("p (c i j) -> p c j i", i=4, j=PACK)

    def part(n):
        return slice(n * CH, (n + 1) * CH)

    with ExitStack() as stack:
        keep = stack.enter_context(tc.tile_pool(name="keep", bufs=1))
        loads = stack.enter_context(tc.tile_pool(name="loads", bufs=4))
        work = stack.enter_context(tc.tile_pool(name="work", bufs=2))
        psum = stack.enter_context(tc.psum_pool(name="psum", bufs=1))
        stack.enter_context(tc.manual_schedule())

        x_codes = keep.tile([P, PASSES, N_IN], U32, align_bytes=64)
        x_scales = keep.tile([P, PASSES, N_IN], U8, align_bytes=64)
        c0_tile = keep.tile([BATCH, H], BF16)
        identity = keep.tile([P, P], F32)
        make_identity(nc, identity[:])

        tiles = [{} for k in range(CHUNKS)]
        codes = {}
        scales = {}
        x_tiles = [{} for g in range(PASSES)]

        def load(k, names):
            if k >= CHUNKS:
                return
            rnd, g = divmod(k, PASSES)
            for name in names:
                loaded = loads.tile(
                    [P, PACK, H_ROUND], dram[name].dtype, name="loaded_" + name, bufs=LOAD_BUFS[name]
                )
                nc.sync.dma_start(
                    out=loaded[:],
                    in_=by_partition(
                        dram[name][g * K_PASS : (g + 1) * K_PASS, rnd * H_ROUND : (rnd + 1) * H_ROUND]
                    ),
                )
                tiles[k]["loaded_" + name] = loaded

        def load_x(g):
            loaded = loads.tile([P, PACK, N_IN], BF16, name="loaded_x", bufs=3)
            nc.sync.dma_start(out=loaded[:], in_=by_partition(x_rows[g * K_PASS : (g + 1) * K_PASS, :]))
            x_tiles[g]["loaded"] = loaded

        def activate(k, out_ap, gate, func):
            nc.scalar.activation(
                out=words_by_four(out_ap), in_=loaded_by_four(tiles[k]["loaded_" + gate][:]), func=func
            )

        def gate_f(k):
            tiles[k]["fi"] = work.tile([P, 2 * CH], F32, name="fi", bufs=4)
            tiles[k]["ug"] = work.tile([P, 2 * CH], F32, name="ug", bufs=4)
            activate(k, tiles[k]["fi"][:, part(0)], "f", ACT.Sigmoid)

        def f_minus_one(k):
            t = tiles[k]
            t["fm1"] = work.tile([P, G_COLS], F32, name="fm1", bufs=4)
            nc.scalar.activation(
                out=t["fm1"][:], in_=t["fi"][:, 0:G_COLS], func=ACT.Identity, bias=-1.0
            )

        def gate_i(k):
            activate(k, tiles[k]["fi"][:, part(1)], "i", ACT.Sigmoid)

        def gate_g(k):
            activate(k, tiles[k]["ug"][:, part(1)], "g", ACT.Tanh)

        def gate_o(k):
            tiles[k]["go"] = work.tile([P, 2 * CH], F32, name="go", bufs=5)
            activate(k, tiles[k]["go"][:, part(1)], "o", ACT.Sigmoid)

        def square_g(k):
            t = tiles[k]
            nc.scalar.activation(out=t["go"][:, part(0)], in_=t["ug"][:, part(1)], func=ACT.Square)

        def tanh_c(k):
            t = tiles[k]
            t["ntc"] = work.tile([P, CH], F32, name="ntc", bufs=3)
            nc.scalar.activation(out=t["ntc"][:], in_=t["c"][:], func=ACT.Tanh, scale=-1.0)

        def square_tanh(k):
            t = tiles[k]
            t["tc2"] = work.tile([P, CH], F32, name="tc_squared", bufs=3)
            nc.scalar.activation(out=t["tc2"][:], in_=t["ntc"][:], func=ACT.Square)

        def product_u(k, engine):
            t = tiles[k]
            columns = slice(k // PASSES * H_ROUND, (k // PASSES + 1) * H_ROUND)
            engine.tensor_tensor(
                out=as_words(t["ug"][:, part(0)]),
                in0=as_words(t["fi"][:, part(0)]),
                in1=c0_tile[:, columns].unsqueeze(2).to_broadcast([P, H_ROUND, PACK]),
                op=ALU.mult,
            )

        def product_w(k, engine):
            t = tiles[k]
            engine.tensor_tensor(
                out=as_words(t["fi"][:, part(0)]),
                in0=as_words(t["go"][:, part(1)]),
                in1=tokens_innermost(t["loaded_grad"][:]),
                op=ALU.mult,
            )

        def minus_one_times(out_ap, in0, in1):
            nc.vector.scalar_tensor_tensor(
                out=out_ap, in0=in0, scalar=1.0, in1=in1, op0=ALU.subtract, op1=ALU.mult
            )

        def times(out_ap, in0, in1):
            nc.vector.tensor_tensor(out=out_ap, in0=in0, in1=in1, op=ALU.mult)

        def factors(k):
            t = tiles[k]
            t["p"] = work.tile([P, 2 * CH], F32, name="factors", bufs=3)
            first = G_COLS if FIRST_G <= k < CHUNKS - 1 else 0
            for columns in (slice(first, CH), part(1)):
                minus_one_times(t["p"][:, columns], t["fi"][:, columns], t["ug"][:, columns])

        def factors_on_gpsimd(k):
            t = tiles[k]
            nc.gpsimd.tensor_tensor(
                out=t["p"][:, 0:G_COLS], in0=t["fm1"][:], in1=t["ug"][:, 0:G_COLS], op=ALU.mult
            )

        def turned(source, name):
            bank = psum.tile([P, CH], F32, name=name, bufs=1)
            for b in range(BLOCKS):
                cols = slice(b * P, (b + 1) * P)
                nc.tensor.transpose(out=bank[:, cols], in_=source[:, cols], identity=identity[:])
            return bank

        def turn_w(k):
            tiles[k]["w_bank"] = turned(tiles[k]["fi"][:, part(0)], "w_bank")

        def turn_i(k):
            tiles[k]["i_bank"] = turned(tiles[k]["fi"][:, part(1)], "i_bank")

        def turn_back(k):
            for name in ("eo", "ndc", "eg"):
                tiles[k][name + "_bank"] = turned(tiles[k][name], name + "_bank")

        def c_bank(k):
            t = tiles[k]
            t["c"] = psum.tile([P, CH], F32, name="c_bank", bufs=1)
            for b in range(BLOCKS):
                terms = (
                    t["ug"][:, b * P : (b + 1) * P],
                    t["ug"][:, CH + b * P : CH + (b + 1) * P],
                    t["p"][:, CH + b * P : CH + (b + 1) * P],
                )
                for n, term in enumerate(terms):
                    nc.tensor.matmul(
                        out=t["c"][:, b * P : (b + 1) * P],
                        lhsT=term,
                        rhs=identity[:],
                        is_transpose=True,
                        start=(n == 0),
                        stop=(n == len(terms) - 1),
                    )

        def turned_product(k, name):
            t = tiles[k]
            t[name] = work.tile([P, CH], F32, name=name, bufs=2)
            if name == "ndc":
                minus_one_times(t["ndc"][:], t["tc2"][:], t["w_bank"][:])
            elif name == "eo":
                times(t["eo"][:], t["ntc"][:], t["w_bank"][:])
            else:
                times(t["eg"][:], t["ndc"][:], t["i_bank"][:])

        def new_da(k):
            tiles[k]["da"] = work.tile([P, 4 * CH], BF16, name="da", bufs=2, align_bytes=64)

        def finish_gate(k, q):
            t = tiles[k]
            da = t["da"][:, part(q)]
            if q == 0:
                times(da, t["p"][:, part(0)], t["ndc_bank"][:])
            elif q == 1:
                times(da, t["p"][:, part(1)], t["eg_bank"][:])
            elif q == 2:
                minus_one_times(da, t["go"][:, part(0)], t["eg_bank"][:])
            else:
                minus_one_times(da, t["go"][:, part(1)], t["eo_bank"][:])

        def copy_ndc(k):
            t = tiles[k]
            t["ndc_copy"] = work.tile([P, CH], F32, name="ndc_copy", bufs=2)
            nc.scalar.copy(out=t["ndc_copy"][:], in_=t["ndc_bank"][:])

        def finish_f_on_gpsimd(k):
            t = tiles[k]
            nc.gpsimd.tensor_tensor(
                out=t["da"][:, part(0)], in0=t["p"][:, part(0)], in1=t["ndc_copy"][:], op=ALU.mult
            )

        def quantise_part(k, first, last):
            rnd, g = divmod(k, PASSES)
            if rnd not in codes:
                codes[rnd] = work.tile([P, PASSES, CH], U32, name="codes", bufs=3, align_bytes=64)
                scales[rnd] = work.tile([P, PASSES, CH], U8, name="scales", bufs=3, align_bytes=64)
            columns = slice(first * H_ROUND, last * H_ROUND)
            nc.vector.quantize_mx(
                out=codes[rnd][:, g, columns].bitcast(E5M2_X4),
                scales=scales[rnd][:, g, columns],
                in_=tiles[k]["da"][:, first * CH : last * CH],
            )

        def x_piece(m):
            g, half = divmod(m, 2)
            cols = N_IN // 2
            if half == 0:
                x_tiles[g]["words"] = work.tile([P, N_IN * PACK], BF16, name="x_words", bufs=2, align_bytes=64)
            nc.scalar.copy(
                out=words_by_four(x_tiles[g]["words"][:, half * cols * PACK : (half + 1) * cols * PACK]),
                in_=loaded_by_four(x_tiles[g]["loaded"][:, :, half * cols : (half + 1) * cols]),
            )

        def x_quantise(g):
            nc.vector.quantize_mx(
                out=x_codes[:, g, :].bitcast(E4M3_X4), scales=x_scales[:, g, :], in_=x_tiles[g]["words"][:]
            )

        def add_passes(acc, rnd, q, passes):
            m_cols = slice(q * H_ROUND, (q + 1) * H_ROUND)
            for g in passes:
                nc.tensor.matmul_mx(
                    out=acc[:],
                    lhsT=codes[rnd][:, g, m_cols].bitcast(E5M2_X4),
                    lhsT_scale=scales[rnd][:, g, m_cols],
                    rhs=x_codes[:, g, :].bitcast(E4M3_X4),
                    rhs_scale=x_scales[:, g, :],
                    start=(g == 0),
                    stop=(g == PASSES - 1),
                )

        def store(rnd, q, acc, copy, dma_start):
            result = work.tile([P, N_IN], F32, name="result", bufs=4)
            copy(out=result[:], in_=acc[:])
            first = GATES.index(DA_ORDER[q]) * H + rnd * H_ROUND
            dma_start(out=out[first : first + H_ROUND, :], in_=result[:])

        zero = keep.tile([P, 1], F32)
        half_tile = keep.tile([P, 1], F32)
        nc.vector.memset(zero[:], 0.0)
        nc.scalar.activation(out=half_tile[:], in_=zero[:], func=ACT.Sigmoid)

        load(0, ("f",))
        nc.sync.dma_start(out=c0_tile[:], in_=c0[:, :])
        load(0, ("i", "g"))
        load(1, ("f",))
        load(0, ("o", "grad"))
        load(1, ("i", "g", "o", "grad"))
        load(2, ("f", "i", "g", "o", "grad"))
        load(3, ("f", "i", "g", "o", "grad"))
        load_x(0)
        load(4, ("f", "i", "g", "o", "grad"))
        load(5, ("f", "i", "g", "o", "grad"))

        gate_f(0)
        gate_i(0)
        gate_g(0)
        product_u(0, nc.vector)
        factors(0)
        c_bank(0)
        turn_i(0)
        gate_f(1)
        product_u(1, nc.vector)
        gate_o(0)
        product_w(0, nc.vector)
        turn_w(0)
        gate_i(1)
        gate_g(1)
        factors(1)
        c_bank(1)
        tanh_c(0)
        square_tanh(0)
        gate_o(1)
        gate_f(2)
        gate_i(2)
        gate_g(2)
        tanh_c(1)
        gate_o(2)
        square_g(0)
        square_tanh(1)
        turned_product(0, "eo")
        turned_product(0, "ndc")
        product_w(1, nc.vector)
        product_u(2, nc.vector)
        turned_product(0, "eg")
        turn_back(0)

        waiting = []
        acc = None
        accs = {}
        for k in range(CHUNKS - 1):
            load(k + 6, ("f", "i", "g", "o", "grad"))
            if k % 2 == 0 and k // 2 + 1 < PASSES:
                load_x(k // 2 + 1)
            if k >= 1:
                quantise_part(k - 1, 0, 4)
                if k % PASSES == 0:
                    waiting.extend([(k // PASSES - 1, q, g) for q in range(4) for g in range(PASSES)])
            if k in GPSIMD_FINISH:
                copy_ndc(k)
            if k + 3 < CHUNKS:
                gate_f(k + 3)
                gate_i(k + 3)
                gate_g(k + 3)
                f_minus_one(k + 3)
            turn_w(k + 1)
            turn_i(k + 1)
            passes = MX_PASSES.get(k, 0)
            for rnd, q, g in waiting[:passes]:
                if g == 0:
                    acc = psum.tile([P, N_IN], F32, name="acc", bufs=2)
                add_passes(acc, rnd, q, (g,))
                if g == PASSES - 1:
                    store(rnd, q, acc, nc.scalar.copy, nc.sync.dma_start)
            waiting = waiting[passes:]
            if k == CHUNKS - 2:
                for q, tag, bufs in ((3, "acc", 2), (0, "acc", 2), (1, "c_bank", 1)):
                    accs[q] = psum.tile([P, N_IN], F32, name=tag, bufs=bufs)
                    add_passes(accs[q], ROUNDS - 1, q, range(PASSES - 2))
            if k + 3 < CHUNKS:
                gate_o(k + 3)
            square_g(k + 1)
            if k + 2 < CHUNKS:
                factors(k + 2)
                c_bank(k + 2)
                tanh_c(k + 2)
            for m in X_PIECES.get(k, ()):
                x_piece(m)
            if k + 2 < CHUNKS:
                square_tanh(k + 2)
            new_da(k)
            for q in (3, 1, 2) if k in GPSIMD_FINISH else (3, 0, 1, 2):
                finish_gate(k, q)
            for name in ("ndc", "eo", "eg"):
                turned_product(k + 1, name)
            turn_back(k + 1)
            if k in X_QUANTISE_STEPS:
                x_quantise(X_QUANTISE_STEPS.index(k))
            if k + 2 < CHUNKS:
                product_w(k + 2, nc.gpsimd)
            if k in GPSIMD_FINISH:
                finish_f_on_gpsimd(k)
            if k + 3 < CHUNKS:
                product_u(k + 3, nc.gpsimd)
            if FIRST_G <= k + 2 < CHUNKS - 1:
                factors_on_gpsimd(k + 2)

        last = CHUNKS - 1
        rnd = ROUNDS - 1
        quantise_part(last - 1, 0, 4)
        for q in (3, 0, 1):
            add_passes(accs[q], rnd, q, (PASSES - 2,))
        accs[2] = psum.tile([P, N_IN], F32, name="w_bank", bufs=1)
        add_passes(accs[2], rnd, 2, range(PASSES - 1))
        new_da(last)
        finish_gate(last, 3)
        finish_gate(last, 0)
        quantise_part(last, 3, 4)
        finish_gate(last, 1)
        quantise_part(last, 0, 1)
        finish_gate(last, 2)
        quantise_part(last, 1, 2)
        quantise_part(last, 2, 3)
        for q in (3, 0, 1, 2):
            add_passes(accs[q], rnd, q, (PASSES - 1,))
        store(rnd, 3, accs[3], nc.scalar.copy, nc.scalar.dma_start)
        store(rnd, 0, accs[0], nc.scalar.copy, nc.sync.dma_start)
        store(rnd, 1, accs[1], nc.scalar.copy, nc.scalar.dma_start)
        store(rnd, 2, accs[2], nc.vector.tensor_copy, nc.sync.dma_start)
